import numpy as np
import ml_dtypes


def mxq(x, axis, fmt="e4m3"):
    dtype, down = {"e4m3": (ml_dtypes.float8_e4m3fn, 7), "e5m2": (ml_dtypes.float8_e5m2, 14)}[fmt]
    v = np.moveaxis(np.asarray(x, np.float32).astype(ml_dtypes.bfloat16).astype(np.float64), axis, -1)
    blocks = v.reshape(v.shape[:-1] + (-1, 32))
    amax = np.abs(blocks).max(-1, keepdims=True)
    byte = np.maximum(np.where(amax > 0, np.frexp(amax)[1] - 1 + 127, 0) - down, 1)
    scale = np.exp2(byte - 127.0)
    codes = (blocks / scale).astype(np.float32).astype(dtype).astype(np.float64)
    return np.moveaxis((codes * scale).reshape(v.shape), -1, axis)


WIDE = False


def mx_kscale(k):
    if not WIDE:
        return np.ones(k)
    levels = np.array([30, -30])
    if k % 512:
        return np.exp2(np.random.permutation(np.resize(levels, k // 32))).repeat(32)
    a = np.empty((k // 512, 16))
    for p in range(k // 512):
        a[p, :8] = np.random.permutation(np.resize(levels, 8))
        for g in range(8):
            far = levels[np.abs(levels - a[p, g]) >= 10]
            a[p, g + 8] = far[np.random.randint(len(far))]
    return np.exp2(a.ravel()).repeat(32)


BF16 = ml_dtypes.bfloat16


def bf(x):
    return np.asarray(x, np.float32).astype(BF16)


def f64(x):
    return np.asarray(x).astype(np.float64)


B, S, D, H, KV, DH, QB = 1, 1024, 1024, 16, 4, 128, 512
HALF = DH // 2
EPS = 1e-6


def rope_tables():
    inv_freq = 1.0 / (10000.0 ** (np.arange(HALF) / HALF))
    ang = np.arange(S)[:, None] * inv_freq[None, :]
    ang = np.concatenate([ang, ang], axis=-1)
    return np.sin(ang), np.cos(ang)


def rmsnorm(u, scale, shift):
    rms = np.sqrt(np.mean(u * u, axis=-1, keepdims=True) + EPS)
    return u / rms * (1.0 + scale) + shift


def apply_rope(u, sin, cos):
    rot = np.concatenate([-u[..., HALF:], u[..., :HALF]], axis=-1)
    return u * cos[None, None, :S, :] + rot * sin[None, None, :S, :]


def heads(u, n):
    return u.reshape(B, S, n, DH).transpose(0, 2, 1, 3)


def setup_inputs():
    s = mx_kscale(D)
    sin, cos = rope_tables()
    return {"x": bf(np.random.standard_normal((B, S, D)) * s),
            "sin_thetas": bf(sin), "cos_thetas": bf(cos),
            "wq": bf(np.random.standard_normal((H * DH, D)) / np.sqrt(D) / s),
            "wk": bf(np.random.standard_normal((KV * DH, D)) / np.sqrt(D) / s),
            "wv": bf(np.random.standard_normal((KV * DH, D)) * 2.0 / np.sqrt(D) / s),
            "q_scale": bf(np.random.standard_normal(DH) * 0.1), "q_shift": bf(np.random.standard_normal(DH) * 0.1),
            "k_scale": bf(np.random.standard_normal(DH) * 0.1), "k_shift": bf(np.random.standard_normal(DH) * 0.1)}


def reference(x, sin_thetas, cos_thetas, wq, wk, wv, q_scale, q_shift, k_scale, k_shift):
    xq = mxq(f64(x), 2, "e5m2")
    q = heads(xq @ mxq(f64(wq), 1, "e4m3").T, H)
    k = heads(xq @ mxq(f64(wk), 1, "e4m3").T, KV)
    v = heads(xq @ mxq(f64(wv), 1, "e4m3").T, KV)
    q = rmsnorm(q, f64(q_scale), f64(q_shift))
    k = rmsnorm(k, f64(k_scale), f64(k_shift))
    q = apply_rope(q, f64(sin_thetas), f64(cos_thetas))
    k = apply_rope(k, f64(sin_thetas), f64(cos_thetas))
    return q, k, v

@@ -1,0 +1,415 @@
+from contextlib import ExitStack
+
+import concourse.mybir as mybir
+from concourse.masks import make_identity
+
+S, D, H, KV, DH = 1024, 1024, 16, 4, 128
+HALF = DH // 2
+EPS = 1e-6
+FLOPS = 2 * S * D * (H + 2 * KV) * DH
+
+F32 = mybir.dt.float32
+BF16 = mybir.dt.bfloat16
+U32 = mybir.dt.uint32
+U8 = mybir.dt.uint8
+E5M2X4 = mybir.dt.float8_e5m2_x4
+E4M3X4 = mybir.dt.float8_e4m3fn_x4
+ACT = mybir.ActivationFunctionType
+ALU = mybir.AluOpType
+
+P = 128
+PASSES = 2
+TILES = S // P
+HG = 4
+NCOL = HG * DH
+WORDS = 256
+
+
+def tile_groupqueryattention_pa_kernel(
+    tc, x, sin_thetas, cos_thetas, wq, wk, wv, q_scale, q_shift, k_scale, k_shift, out_0, out_1, out_2
+):
+    nc = tc.nc
+    with ExitStack() as ctx:
+        keep = ctx.enter_context(tc.tile_pool(name="keep", bufs=1))
+        work = ctx.enter_context(tc.tile_pool(name="work", bufs=2))
+        psum = ctx.enter_context(tc.psum_pool(name="psum", bufs=6))
+        psum_keep = ctx.enter_context(tc.psum_pool(name="psum_keep", bufs=1))
+        ctx.enter_context(tc.manual_schedule())
+
+        groups = ["q0", "q1", "q2", "q3", "k", "v"]
+        w_rows = {"q%d" % g: wq[g * NCOL : (g + 1) * NCOL, :] for g in range(4)}
+        w_rows["k"] = wk
+        w_rows["v"] = wv
+        out_q = out_0[0].rearrange("h (p t) d -> p h t d", t=TILES)
+        out_of = {"q%d" % g: out_q[:, g * HG : (g + 1) * HG] for g in range(4)}
+        out_of["k"] = out_1[0].rearrange("h (p t) d -> p h t d", t=TILES)
+        out_of["v"] = out_2[0].rearrange("h (p t) d -> p h t d", t=TILES)
+
+        x_raw = keep.tile([P, TILES, D], BF16, align_bytes=64)
+        w_raw = {g: keep.tile([P, HG, D], BF16, name="w_raw_" + g, align_bytes=64) for g in groups}
+        x_codes = keep.tile([P, TILES, PASSES, P], U32, align_bytes=64)
+        x_scales = keep.tile([P, TILES, PASSES, P], U8, align_bytes=64)
+        w_codes = {g: keep.tile([P, PASSES, NCOL], U32, name="w_codes_" + g, align_bytes=64) for g in groups}
+        w_scales = {g: keep.tile([P, PASSES, NCOL], U8, name="w_scales_" + g, align_bytes=64) for g in groups}
+        cos_sb = keep.tile([P, TILES, DH], BF16)
+        sin_sb = keep.tile([P, TILES, DH], BF16)
+        cos_t = keep.tile([P, TILES, P], BF16)
+        sin_t = keep.tile([P, TILES, P], BF16)
+        vec = keep.tile([P, 4, DH], BF16)
+        ones = keep.tile([P, P], BF16)
+        ident_f32 = keep.tile([P, P], F32)
+        ident_bf = keep.tile([P, P], BF16)
+        gain = {n: keep.tile([P, DH], F32, name="gain_" + n) for n in "qk"}
+        gain_rot = {n: keep.tile([P, DH], F32, name="gain_rot_" + n) for n in "qk"}
+        diag_cos = keep.tile([P, 2, DH], BF16)
+        diag_sin = keep.tile([P, 2, DH], BF16)
+        table = {n: keep.tile([P, TILES, 4, HALF], F32, name="table_" + n) for n in "qk"}
+        shift_sb = {n: keep.tile([P, TILES, DH], F32, name="shift_sb_" + n) for n in "qk"}
+        shift_ps = [psum_keep.tile([P, 4, DH], F32, name="shift_ps_%d" % i) for i in range(2)]
+
+        nc.vector.memset(vec[:], 0.0)
+        nc.vector.memset(ones[:], 1.0)
+        make_identity(nc, ident_f32[:])
+        make_identity(nc, ident_bf[:])
+        for i, row in enumerate((q_scale, q_shift, k_scale, k_shift)):
+            nc.scalar.dma_start(out=vec[0:1, i, :], in_=row.rearrange("(o d) -> o d", o=1))
+        x_view = x[0].rearrange("(p t) k -> p t k", t=TILES)
+
+        def load_x(t0, t1):
+            nc.sync.dma_start(out=x_raw[:, t0:t1, :], in_=x_view[:, t0:t1, :])
+
+        def load_w(g, j0, j1):
+            nc.sync.dma_start(
+                out=w_raw[g][:, j0:j1, :], in_=w_rows[g].rearrange("(j p) k -> p j k", p=P)[:, j0:j1, :]
+            )
+
+        load_x(0, 1)
+        load_w("q0", 0, 2)
+        nc.sync.dma_start(out=cos_sb[:], in_=cos_thetas.rearrange("(p t) d -> p t d", t=TILES))
+        nc.sync.dma_start(out=sin_sb[:], in_=sin_thetas.rearrange("(p t) d -> p t d", t=TILES))
+        load_w("q0", 2, 4)
+        load_x(1, 2)
+        load_x(2, 4)
+        load_x(4, 8)
+        for g in ("q1", "k", "q2", "v", "q3"):
+            load_w(g, 0, HG)
+
+        turned = {}
+        grouped = {}
+
+        def turn_x(t):
+            bank = psum.tile([P, PASSES, 2, P], F32, name="bank", tag="bank")
+            words = x_raw[:, t, :].bitcast(F32)
+            for c in range(PASSES):
+                for u in range(2):
+                    nc.tensor.transpose(
+                        bank[:, c, u, :], words[:, WORDS * c + u : WORDS * (c + 1) : 2], ident_f32[:]
+                    )
+            turned["x", t] = bank
+
+        def empty_x(t):
+            g = work.tile([P, PASSES, P, 2], F32, name="x_grouped", tag="x_grouped", bufs=3, align_bytes=64)
+            nc.scalar.copy(out=g[:], in_=turned["x", t][:].rearrange("p c u r -> p c r u"))
+            grouped["x", t] = g
+
+        def quant_x(t):
+            nc.vector.quantize_mx(
+                out=x_codes[:, t].rearrange("p c r -> p (c r)").bitcast(E5M2X4),
+                scales=x_scales[:, t].rearrange("p c r -> p (c r)"),
+                in_=grouped["x", t][:].rearrange("p c r u -> p (c r u)").bitcast(BF16),
+            )
+
+        def turn_w(g, b):
+            pair, c = divmod(b, PASSES)
+            bank = psum.tile([P, 2, 2, P], F32, name="bank", tag="bank")
+            for j in range(2):
+                words = w_raw[g][:, 2 * pair + j, :].bitcast(F32)
+                for u in range(2):
+                    nc.tensor.transpose(
+                        bank[:, j, u, :], words[:, WORDS * c + u : WORDS * (c + 1) : 2], ident_f32[:]
+                    )
+            turned[g, b] = bank
+
+        def empty_w(g, b):
+            pair, c = divmod(b, PASSES)
+            if b == 0:
+                grouped[g] = work.tile(
+                    [P, PASSES, HG, P, 2], F32, name="w_grouped", tag="w_grouped", bufs=2, align_bytes=64
+                )
+            nc.scalar.copy(
+                out=grouped[g][:, c, 2 * pair : 2 * pair + 2],
+                in_=turned[g, b][:].rearrange("p j u r -> p j r u"),
+            )
+
+        def quant_w_bank(g, b):
+            pair, c = divmod(b, PASSES)
+            cols = slice(2 * pair * P, 2 * (pair + 1) * P)
+            nc.vector.quantize_mx(
+                out=w_codes[g][:, c, cols].bitcast(E4M3X4),
+                scales=w_scales[g][:, c, cols],
+                in_=grouped[g][:, c, 2 * pair : 2 * pair + 2].rearrange("p j r u -> p (j r u)").bitcast(BF16),
+            )
+
+        def quant_w(g):
+            nc.vector.quantize_mx(
+                out=w_codes[g][:].rearrange("p c n -> p (c n)").bitcast(E4M3X4),
+                scales=w_scales[g][:].rearrange("p c n -> p (c n)"),
+                in_=grouped[g][:].rearrange("p c j r u -> p (c j r u)").bitcast(BF16),
+            )
+
+        acc = {}
+
+        def project(g, t):
+            bank = psum.tile([P, HG, DH], F32, name="bank", tag="bank")
+            for c in range(PASSES):
+                nc.tensor.matmul_mx(
+                    out=bank[:].rearrange("p h d -> p (h d)"),
+                    lhsT=x_codes[:, t, c, :].bitcast(E5M2X4),
+                    lhsT_scale=x_scales[:, t, c, :],
+                    rhs=w_codes[g][:, c, :].bitcast(E4M3X4),
+                    rhs_scale=w_scales[g][:, c, :],
+                    start=(c == 0),
+                    stop=(c == PASSES - 1),
+                )
+            acc[g, t] = bank
+
+        spread = psum.tile([P, 4, DH], F32, name="bank", tag="bank")
+
+        def make_gains(n):
+            s = spread[:, 0 if n == "q" else 2, :]
+            nc.vector.tensor_scalar(out=gain[n][:], in0=s, scalar1=1.0, scalar2=None, op0=ALU.add)
+            nc.vector.tensor_scalar(
+                out=gain_rot[n][:, :HALF], in0=s[:, HALF:], scalar1=-1.0, scalar2=-1.0, op0=ALU.mult, op1=ALU.add
+            )
+            nc.vector.tensor_scalar(
+                out=gain_rot[n][:, HALF:], in0=s[:, :HALF], scalar1=1.0, scalar2=None, op0=ALU.add
+            )
+
+        def make_diags():
+            shifts = spread[:, 1:4:2, :]
+            nc.vector.tensor_tensor(
+                out=diag_cos[:], in0=shifts, in1=ident_bf[:].unsqueeze(1).to_broadcast([P, 2, DH]), op=ALU.mult
+            )
+            nc.vector.scalar_tensor_tensor(
+                out=diag_sin[:, :, :HALF],
+                in0=shifts[:, :, HALF:],
+                scalar=-1.0,
+                in1=ident_bf[:, :HALF].unsqueeze(1).to_broadcast([P, 2, HALF]),
+                op0=ALU.mult,
+                op1=ALU.mult,
+            )
+            nc.vector.tensor_tensor(
+                out=diag_sin[:, :, HALF:],
+                in0=shifts[:, :, :HALF],
+                in1=ident_bf[:, HALF:].unsqueeze(1).to_broadcast([P, 2, HALF]),
+                op=ALU.mult,
+            )
+
+        def table_cos(engine, n, t0, t1):
+            engine.tensor_tensor(
+                out=table[n][:, t0:t1, 0:4:3, :],
+                in0=cos_sb[:, t0:t1, :].rearrange("p t (j e) -> p t j e", j=2),
+                in1=gain[n][:].rearrange("p (j e) -> p j e", j=2).unsqueeze(1).to_broadcast([P, t1 - t0, 2, HALF]),
+                op=ALU.mult,
+            )
+
+        def table_sin(engine, n, t0, t1):
+            engine.tensor_tensor(
+                out=table[n][:, t0:t1, 1:3, :].rearrange("p t j e -> p t (j e)"),
+                in0=sin_sb[:, t0:t1, :],
+                in1=gain_rot[n][:].unsqueeze(1).to_broadcast([P, t1 - t0, DH]),
+                op=ALU.mult,
+            )
+
+        def turn_trig(name, src):
+            bank = psum.tile([P, TILES, P], BF16, name="bank", tag="bank")
+            for t in range(TILES):
+                nc.tensor.transpose(bank[:, t, :], src[:, t, :], ident_bf[:])
+            turned[name] = bank
+
+        def rotate_shift(n, half, bank):
+            i = 0 if n == "q" else 1
+            for tt in range(4):
+                t = 4 * half + tt
+                nc.tensor.matmul(bank[:, tt, :], lhsT=cos_t[:, t, :], rhs=diag_cos[:, i, :], start=True, stop=False)
+                nc.tensor.matmul(bank[:, tt, :], lhsT=sin_t[:, t, :], rhs=diag_sin[:, i, :], start=False, stop=True)
+
+        def rotate_shift_k(half):
+            bank = psum.tile([P, 4, DH], F32, name="bank", tag="bank")
+            rotate_shift("k", half, bank)
+            turned["shift_k", half] = bank
+
+        sums = {}
+        rstd = {}
+        prods = {}
+        stage = {}
+
+        def squares(g, t):
+            junk = work.tile([P, HG, DH], BF16, name="junk", tag="junk", bufs=2)
+            ss = work.tile([P, HG], F32, name="ss", tag="ss", bufs=4)
+            for h in range(HG):
+                nc.scalar.activation(
+                    out=junk[:, h, :], in_=acc[g, t][:, h, :], func=ACT.Square, accum_out=ss[:, h : h + 1]
+                )
+            sums[g, t] = ss
+
+        def inverse_rms(g, t):
+            r = work.tile([P, HG], F32, name="r", tag="r", bufs=4)
+            nc.scalar.activation(
+                out=r[:], in_=sums[g, t][:], func=ACT.Abs_reciprocal_sqrt, scale=1.0 / DH, bias=EPS
+            )
+            rstd[g, t] = r
+
+        def multiply(g, t):
+            pr = work.tile([P, HG, 2, 2, HALF], F32, name="pr", tag="pr", bufs=5)
+            for h in range(HG):
+                nc.vector.scalar_tensor_tensor(
+                    out=pr[:, h].rearrange("p j s e -> p j (s e)"),
+                    in0=acc[g, t][:, h, :].unsqueeze(1).to_broadcast([P, 2, DH]),
+                    scalar=rstd[g, t][:, h : h + 1],
+                    in1=table[g[0]][:, t].rearrange("p (j s) e -> p j (s e)", j=2),
+                    op0=ALU.mult,
+                    op1=ALU.mult,
+                )
+            prods[g, t] = pr
+
+        def staged(g, t):
+            if t % 2 == 0:
+                stage[g, t // 2] = work.tile([P, HG, 2, DH], F32, name="stage", tag="stage", bufs=8)
+            return staged_view(g, t)
+
+        def staged_view(g, t):
+            return stage[g, t // 2][:, :, t % 2, :].rearrange("p h (j e) -> p h j e", j=2)
+
+        def add_shift(engine, g, t, shift):
+            engine.tensor_tensor(
+                out=staged(g, t),
+                in0=prods[g, t][:, :, :, 0, :],
+                in1=shift.rearrange("p (j e) -> p j e", j=2).unsqueeze(1).to_broadcast([P, HG, 2, HALF]),
+                op=ALU.add,
+            )
+
+        def add_second(engine, g, t):
+            engine.tensor_tensor(
+                out=staged_view(g, t), in0=staged_view(g, t), in1=prods[g, t][:, :, :, 1, :], op=ALU.add
+            )
+
+        def store(g, t, single):
+            if single:
+                nc.sync.dma_start(out=out_of[g][:, :, t, :], in_=stage[g, t // 2][:, :, t % 2, :])
+            elif t % 2 == 1:
+                nc.sync.dma_start(
+                    out=out_of[g][:, :, t - 1 : t + 1, :].rearrange("p h t d -> p h (t d)"),
+                    in_=stage[g, t // 2][:].rearrange("p h t d -> p h (t d)"),
+                )
+
+        def empty_v(t):
+            nc.scalar.copy(out=staged("v", t), in_=acc["v", t][:].rearrange("p h (j e) -> p h j e", j=2))
+
+        steps = []
+        q_left = [("q%d" % g, t) for g in range(4) for t in range(TILES)]
+        k_left = [("k", t) for t in range(TILES)]
+        for s in range(5 * TILES):
+            steps.append(k_left.pop(0) if (s >= 14 and s % 3 == 2 and k_left) else q_left.pop(0))
+        n_steps = len(steps)
+
+        def pool_adds_both(s):
+            return s % 3 == 2 and s < n_steps - 3
+
+        turn_x(0)
+        empty_x(0)
+        nc.tensor.matmul(
+            spread[:].rearrange("p a d -> p (a d)"),
+            lhsT=ones[:],
+            rhs=vec[:].rearrange("p a d -> p (a d)"),
+            start=True,
+            stop=True,
+        )
+        make_gains("q")
+        make_diags()
+        quant_x(0)
+        for b in range(2):
+            turn_w("q0", b)
+            empty_w("q0", b)
+        table_cos(nc.vector, "q", 0, TILES)
+        quant_w_bank("q0", 0)
+        quant_w_bank("q0", 1)
+        table_sin(nc.vector, "q", 0, TILES)
+        for b in range(2, 4):
+            turn_w("q0", b)
+            empty_w("q0", b)
+            quant_w_bank("q0", b)
+        make_gains("k")
+        turn_x(1)
+        empty_x(1)
+        turn_trig("cos", cos_sb)
+        nc.scalar.copy(out=cos_t[:], in_=turned["cos"][:])
+        project(*steps[0])
+        quant_x(1)
+        turn_trig("sin", sin_sb)
+        for t0 in range(0, TILES, 2):
+            table_cos(nc.gpsimd, "k", t0, t0 + 2)
+            table_sin(nc.gpsimd, "k", t0, t0 + 2)
+        turn_x(2)
+        squares(*steps[0])
+        nc.scalar.copy(out=sin_t[:], in_=turned["sin"][:])
+        inverse_rms(*steps[0])
+        empty_x(2)
+        project(*steps[1])
+        quant_x(2)
+        rotate_shift("q", 0, shift_ps[0])
+        rotate_shift("q", 1, shift_ps[1])
+        turn_x(3)
+
+        turns = {0: [("x", 4)], 1: [("x", 5), ("q1", 0)], 2: [("x", 6), ("q1", 1)], 3: [("x", 7), ("q1", 2), ("q1", 3)]}
+        first_turn = {"k": 5, "q2": 10, "v": 14, "q3": 18}
+        for g, s0 in first_turn.items():
+            for b in range(4):
+                turns[s0 + b] = [(g, b)]
+        turns[-1] = [("x", 3)]
+        v_slot = {22 + 2 * t: t for t in range(TILES)}
+
+        for s in range(n_steps + 1):
+            if s + 2 < n_steps:
+                project(*steps[s + 2])
+            if s in v_slot:
+                project("v", v_slot[s])
+            for g, b in turns.get(s, []):
+                if g == "x":
+                    turn_x(b)
+                else:
+                    turn_w(g, b)
+            if s in (9, 10):
+                rotate_shift_k(s - 9)
+            if s + 1 < n_steps:
+                squares(*steps[s + 1])
+            for g, b in turns.get(s - 1, []):
+                if g == "x":
+                    empty_x(b)
+                else:
+                    empty_w(g, b)
+            if s in (10, 11):
+                nc.scalar.copy(out=shift_sb["k"][:, 4 * (s - 10) : 4 * (s - 9), :], in_=turned["shift_k", s - 10][:])
+            if s - 1 in v_slot:
+                empty_v(v_slot[s - 1])
+                store("v", v_slot[s - 1], False)
+            if s + 1 < n_steps:
+                inverse_rms(*steps[s + 1])
+            if s in (1, 3):
+                nc.scalar.copy(out=shift_sb["q"][:, 2 * (s - 1) : 2 * (s + 1), :], in_=shift_ps[(s - 1) // 2][:])
+            if s < n_steps:
+                multiply(*steps[s])
+            for g, b in turns.get(s - 1, []):
+                if g == "x":
+                    quant_x(b)
+                elif b == 3:
+                    quant_w(g)
+            if s >= 1:
+                g, t = steps[s - 1]
+                last = s - 1 >= n_steps - 2
+                if pool_adds_both(s - 1):
+                    add_shift(nc.gpsimd, g, t, shift_sb[g[0]][:, t, :])
+                else:
+                    add_shift(nc.vector, g, t, shift_ps[t // 4][:, t % 4, :])
+                add_second(nc.vector if s == n_steps else nc.gpsimd, g, t)
+                store(g, t, last)

@@ -23,6 +23,17 @@ TILES = S // P
 HG = 4
 NCOL = HG * DH
 WORDS = 256
+N_TENSOR_ADDS = 8
+K_AFTER_PAIRS = (4, 6, 8, 9, 10, 11, 12, 13)
+POOL_PAIRS = (4, 6, 8, 10, 12, 13)
+PR_BUFS = 3
+W_ORDER = ("q1", "k", "q2", "v", "q3")
+V_FIRST = 19
+V_STEP = 2
+MX_AHEAD = 2
+LAG = 1
+LATE_TURNS = (5, 8, 14)
+LATE_QUANTS = (5, 7, 9)
 
 
 def tile_groupqueryattention_pa_kernel(
@@ -32,7 +43,7 @@ def tile_groupqueryattention_pa_kernel(
     with ExitStack() as ctx:
         keep = ctx.enter_context(tc.tile_pool(name="keep", bufs=1))
         work = ctx.enter_context(tc.tile_pool(name="work", bufs=2))
-        psum = ctx.enter_context(tc.psum_pool(name="psum", bufs=6))
+        psum = ctx.enter_context(tc.psum_pool(name="psum", bufs=7))
         psum_keep = ctx.enter_context(tc.psum_pool(name="psum_keep", bufs=1))
         ctx.enter_context(tc.manual_schedule())
 
@@ -53,26 +64,23 @@ def tile_groupqueryattention_pa_kernel(
         w_scales = {g: keep.tile([P, PASSES, NCOL], U8, name="w_scales_" + g, align_bytes=64) for g in groups}
         cos_sb = keep.tile([P, TILES, DH], BF16)
         sin_sb = keep.tile([P, TILES, DH], BF16)
-        cos_t = keep.tile([P, TILES, P], BF16)
-        sin_t = keep.tile([P, TILES, P], BF16)
+        trig = keep.tile([P, TILES, 4, HALF], BF16)
+        trig_t = keep.tile([P, 2, TILES, P], BF16)
         vec = keep.tile([P, 4, DH], BF16)
         ones = keep.tile([P, P], BF16)
         ident_f32 = keep.tile([P, P], F32)
         ident_bf = keep.tile([P, P], BF16)
-        gain = {n: keep.tile([P, DH], F32, name="gain_" + n) for n in "qk"}
-        gain_rot = {n: keep.tile([P, DH], F32, name="gain_rot_" + n) for n in "qk"}
-        diag_cos = keep.tile([P, 2, DH], BF16)
-        diag_sin = keep.tile([P, 2, DH], BF16)
+        gain = {n: keep.tile([P, 2, DH], F32, name="gain_" + n) for n in "qk"}
+        diag = keep.tile([P, 2, DH], BF16)
+        fold = keep.tile([P, 2, 2, HALF], BF16)
         table = {n: keep.tile([P, TILES, 4, HALF], F32, name="table_" + n) for n in "qk"}
-        shift_sb = {n: keep.tile([P, TILES, DH], F32, name="shift_sb_" + n) for n in "qk"}
-        shift_ps = [psum_keep.tile([P, 4, DH], F32, name="shift_ps_%d" % i) for i in range(2)]
+        shift_sb = {n: keep.tile([P, TILES, DH], F32, name="shift_sb_" + n) for n in "q"}
+        shift_ps = {1: psum_keep.tile([P, 2, 2, DH], F32, name="shift_ps_odd")}
 
         nc.vector.memset(vec[:], 0.0)
         nc.vector.memset(ones[:], 1.0)
         make_identity(nc, ident_f32[:])
         make_identity(nc, ident_bf[:])
-        for i, row in enumerate((q_scale, q_shift, k_scale, k_shift)):
-            nc.scalar.dma_start(out=vec[0:1, i, :], in_=row.rearrange("(o d) -> o d", o=1))
         x_view = x[0].rearrange("(p t) k -> p t k", t=TILES)
 
         def load_x(t0, t1):
@@ -84,6 +92,8 @@ def tile_groupqueryattention_pa_kernel(
             )
 
         load_x(0, 1)
+        for i, row in enumerate((q_scale, q_shift, k_scale, k_shift)):
+            nc.sync.dma_start(out=vec[0:1, i, :], in_=row.rearrange("(o d) -> o d", o=1))
         load_w("q0", 0, 2)
         nc.sync.dma_start(out=cos_sb[:], in_=cos_thetas.rearrange("(p t) d -> p t d", t=TILES))
         nc.sync.dma_start(out=sin_sb[:], in_=sin_thetas.rearrange("(p t) d -> p t d", t=TILES))
@@ -91,7 +101,7 @@ def tile_groupqueryattention_pa_kernel(
         load_x(1, 2)
         load_x(2, 4)
         load_x(4, 8)
-        for g in ("q1", "k", "q2", "v", "q3"):
+        for g in W_ORDER:
             load_w(g, 0, HG)
 
         turned = {}
@@ -107,16 +117,18 @@ def tile_groupqueryattention_pa_kernel(
                     )
             turned["x", t] = bank
 
-        def empty_x(t):
-            g = work.tile([P, PASSES, P, 2], F32, name="x_grouped", tag="x_grouped", bufs=3, align_bytes=64)
-            nc.scalar.copy(out=g[:], in_=turned["x", t][:].rearrange("p c u r -> p c r u"))
-            grouped["x", t] = g
+        def empty_x(t, copy=nc.scalar.copy):
+            if t % 2 == 0:
+                grouped["x", t // 2] = work.tile(
+                    [P, 2, PASSES, P, 2], F32, name="x_grouped", tag="x_grouped", bufs=2, align_bytes=64
+                )
+            copy(out=grouped["x", t // 2][:, t % 2], in_=turned["x", t][:].rearrange("p c u r -> p c r u"))
 
-        def quant_x(t):
+        def quant_x(t, n=1):
             nc.vector.quantize_mx(
-                out=x_codes[:, t].rearrange("p c r -> p (c r)").bitcast(E5M2X4),
-                scales=x_scales[:, t].rearrange("p c r -> p (c r)"),
-                in_=grouped["x", t][:].rearrange("p c r u -> p (c r u)").bitcast(BF16),
+                out=x_codes[:, t : t + n].rearrange("p t c r -> p (t c r)").bitcast(E5M2X4),
+                scales=x_scales[:, t : t + n].rearrange("p t c r -> p (t c r)"),
+                in_=grouped["x", t // 2][:, t % 2 : t % 2 + n].rearrange("p t c r u -> p (t c r u)").bitcast(BF16),
             )
 
         def turn_w(g, b):
@@ -134,7 +146,7 @@ def tile_groupqueryattention_pa_kernel(
             pair, c = divmod(b, PASSES)
             if b == 0:
                 grouped[g] = work.tile(
-                    [P, PASSES, HG, P, 2], F32, name="w_grouped", tag="w_grouped", bufs=2, align_bytes=64
+                    [P, PASSES, HG, P, 2], F32, name="w_grouped", tag="w_grouped", bufs=3, align_bytes=64
                 )
             nc.scalar.copy(
                 out=grouped[g][:, c, 2 * pair : 2 * pair + 2],
@@ -175,69 +187,75 @@ def tile_groupqueryattention_pa_kernel(
 
         spread = psum.tile([P, 4, DH], F32, name="bank", tag="bank")
 
-        def make_gains(n):
-            s = spread[:, 0 if n == "q" else 2, :]
-            nc.vector.tensor_scalar(out=gain[n][:], in0=s, scalar1=1.0, scalar2=None, op0=ALU.add)
+        def gain_part(n, lo, hi, src, sign):
+            s = spread[:, 2 * "qk".index(n), :]
             nc.vector.tensor_scalar(
-                out=gain_rot[n][:, :HALF], in0=s[:, HALF:], scalar1=-1.0, scalar2=-1.0, op0=ALU.mult, op1=ALU.add
-            )
-            nc.vector.tensor_scalar(
-                out=gain_rot[n][:, HALF:], in0=s[:, :HALF], scalar1=1.0, scalar2=None, op0=ALU.add
-            )
-
-        def make_diags():
-            shifts = spread[:, 1:4:2, :]
-            nc.vector.tensor_tensor(
-                out=diag_cos[:], in0=shifts, in1=ident_bf[:].unsqueeze(1).to_broadcast([P, 2, DH]), op=ALU.mult
-            )
-            nc.vector.scalar_tensor_tensor(
-                out=diag_sin[:, :, :HALF],
-                in0=shifts[:, :, HALF:],
-                scalar=-1.0,
-                in1=ident_bf[:, :HALF].unsqueeze(1).to_broadcast([P, 2, HALF]),
+                out=gain[n][:].rearrange("p j d -> p (j d)")[:, lo:hi],
+                in0=s[:, src : src + hi - lo],
+                scalar1=sign,
+                scalar2=sign,
                 op0=ALU.mult,
-                op1=ALU.mult,
+                op1=ALU.add,
             )
+
+        def make_gains(n):
+            gain_part(n, 0, HALF, 0, 1.0)
+            gain_part(n, HALF, DH, HALF, -1.0)
+            gain_part(n, DH, 2 * DH, 0, 1.0)
+
+        def make_folds():
             nc.vector.tensor_tensor(
-                out=diag_sin[:, :, HALF:],
-                in0=shifts[:, :, :HALF],
-                in1=ident_bf[:, HALF:].unsqueeze(1).to_broadcast([P, 2, HALF]),
+                out=diag[:],
+                in0=spread[:, 1:4:2, :],
+                in1=ident_bf[:].unsqueeze(1).to_broadcast([P, 2, DH]),
                 op=ALU.mult,
             )
+            gain_part("k", 0, HALF, 0, 1.0)
+            gain_part("k", HALF, DH, HALF, -1.0)
+            for j, op in enumerate((ALU.subtract, ALU.add)):
+                nc.vector.tensor_tensor(out=fold[:, :, j, :], in0=diag[:, :, :HALF], in1=diag[:, :, HALF:], op=op)
 
-        def table_cos(engine, n, t0, t1):
+        def arrange_trig():
+            nc.scalar.copy(out=trig[:, :, 0:4:3, :], in_=cos_sb[:].rearrange("p t (j e) -> p t j e", j=2))
+            nc.scalar.copy(out=trig[:, :, 1:3, :].rearrange("p t j e -> p t (j e)"), in_=sin_sb[:])
+
+        def make_table(engine, n, t0, t1):
             engine.tensor_tensor(
-                out=table[n][:, t0:t1, 0:4:3, :],
-                in0=cos_sb[:, t0:t1, :].rearrange("p t (j e) -> p t j e", j=2),
-                in1=gain[n][:].rearrange("p (j e) -> p j e", j=2).unsqueeze(1).to_broadcast([P, t1 - t0, 2, HALF]),
+                out=table[n][:, t0:t1].rearrange("p t a e -> p t (a e)"),
+                in0=trig[:, t0:t1].rearrange("p t a e -> p t (a e)"),
+                in1=gain[n][:].rearrange("p j d -> p (j d)").unsqueeze(1).to_broadcast([P, t1 - t0, 2 * DH]),
                 op=ALU.mult,
             )
 
-        def table_sin(engine, n, t0, t1):
-            engine.tensor_tensor(
-                out=table[n][:, t0:t1, 1:3, :].rearrange("p t j e -> p t (j e)"),
-                in0=sin_sb[:, t0:t1, :],
-                in1=gain_rot[n][:].unsqueeze(1).to_broadcast([P, t1 - t0, DH]),
-                op=ALU.mult,
-            )
-
-        def turn_trig(name, src):
+        def turn_trig(j):
             bank = psum.tile([P, TILES, P], BF16, name="bank", tag="bank")
             for t in range(TILES):
-                nc.tensor.transpose(bank[:, t, :], src[:, t, :], ident_bf[:])
-            turned[name] = bank
+                nc.tensor.transpose(
+                    bank[:, t, :], trig[:, t, 2 * j : 2 * j + 2, :].rearrange("p a e -> p (a e)"), ident_bf[:]
+                )
+            turned["trig", j] = bank
 
-        def rotate_shift(n, half, bank):
-            i = 0 if n == "q" else 1
-            for tt in range(4):
-                t = 4 * half + tt
-                nc.tensor.matmul(bank[:, tt, :], lhsT=cos_t[:, t, :], rhs=diag_cos[:, i, :], start=True, stop=False)
-                nc.tensor.matmul(bank[:, tt, :], lhsT=sin_t[:, t, :], rhs=diag_sin[:, i, :], start=False, stop=True)
+        def rotate_shift(n, t, dst):
+            for j in range(2):
+                nc.tensor.matmul(
+                    dst[:, j * HALF : (j + 1) * HALF],
+                    lhsT=trig_t[:, j, t, :],
+                    rhs=fold[:, "qk".index(n), j, :],
+                    start=True,
+                    stop=True,
+                )
 
-        def rotate_shift_k(half):
+        def shifts_for_pool(n, tiles):
             bank = psum.tile([P, 4, DH], F32, name="bank", tag="bank")
-            rotate_shift("k", half, bank)
-            turned["shift_k", half] = bank
+            for i, t in enumerate(tiles):
+                rotate_shift(n, t, bank[:, i, :])
+            turned["shift", n] = bank
+
+        def empty_shifts(n, tiles):
+            for i, t in enumerate(tiles):
+                if i % 2 == 0:
+                    w = min(2, len(tiles) - i)
+                    nc.scalar.copy(out=shift_sb[n][:, t : t + w, :], in_=turned["shift", n][:, i : i + w, :])
 
         sums = {}
         rstd = {}
@@ -261,7 +279,13 @@ def tile_groupqueryattention_pa_kernel(
             rstd[g, t] = r
 
         def multiply(g, t):
-            pr = work.tile([P, HG, 2, 2, HALF], F32, name="pr", tag="pr", bufs=5)
+            if (g, t) in tensor_steps:
+                prods[g, t] = work.tile([P, HG, 2, 2, HALF], F32, name="pr_one", tag="pr_one", bufs=2)
+                pr = prods[g, t][:]
+            else:
+                if t % 2 == 0:
+                    prods[g, t // 2] = work.tile([P, HG, 2, 2, 2, HALF], F32, name="pr", tag="pr", bufs=PR_BUFS)
+                pr = prods[g, t // 2][:, :, t % 2]
             for h in range(HG):
                 nc.vector.scalar_tensor_tensor(
                     out=pr[:, h].rearrange("p j s e -> p j (s e)"),
@@ -271,28 +295,50 @@ def tile_groupqueryattention_pa_kernel(
                     op0=ALU.mult,
                     op1=ALU.mult,
                 )
-            prods[g, t] = pr
 
         def staged(g, t):
             if t % 2 == 0:
-                stage[g, t // 2] = work.tile([P, HG, 2, DH], F32, name="stage", tag="stage", bufs=8)
+                stage[g, t // 2] = work.tile([P, HG, 2, DH], F32, name="stage", tag="stage", bufs=5)
             return staged_view(g, t)
 
         def staged_view(g, t):
             return stage[g, t // 2][:, :, t % 2, :].rearrange("p h (j e) -> p h j e", j=2)
 
-        def add_shift(engine, g, t, shift):
+        def add_shift(engine, g, pair, shift):
+            stage[g, pair] = work.tile([P, HG, 2, DH], F32, name="stage", tag="stage", bufs=5)
             engine.tensor_tensor(
-                out=staged(g, t),
-                in0=prods[g, t][:, :, :, 0, :],
+                out=stage[g, pair][:].rearrange("p h t (j e) -> p h (t j) e", j=2),
+                in0=prods[g, pair][:, :, :, :, 0, :].rearrange("p h t j e -> p h (t j) e"),
+                in1=shift.rearrange("p t (j e) -> p (t j) e", j=2).unsqueeze(1).to_broadcast([P, HG, 4, HALF]),
+                op=ALU.add,
+            )
+
+        def add_second(engine, g, pair):
+            both = stage[g, pair][:].rearrange("p h t (j e) -> p (h t j) e", j=2)
+            engine.tensor_tensor(
+                out=both,
+                in0=both,
+                in1=prods[g, pair][:, :, :, :, 1, :].rearrange("p h t j e -> p (h t j) e"),
+                op=ALU.add,
+            )
+
+        def add_last(g, t, shift):
+            if t % 2 == 0:
+                stage[g, t // 2] = work.tile([P, HG, 2, DH], F32, name="stage", tag="stage", bufs=5)
+            pr = prods[g, t // 2][:, :, t % 2]
+            nc.vector.tensor_tensor(
+                out=staged_view(g, t),
+                in0=pr[:, :, :, 0, :],
                 in1=shift.rearrange("p (j e) -> p j e", j=2).unsqueeze(1).to_broadcast([P, HG, 2, HALF]),
                 op=ALU.add,
             )
 
-        def add_second(engine, g, t):
-            engine.tensor_tensor(
-                out=staged_view(g, t), in0=staged_view(g, t), in1=prods[g, t][:, :, :, 1, :], op=ALU.add
+        def add_last_second(g, t):
+            pr = prods[g, t // 2][:, :, t % 2]
+            nc.vector.tensor_tensor(
+                out=staged_view(g, t), in0=staged_view(g, t), in1=pr[:, :, :, 1, :], op=ALU.add
             )
+            store(g, t, True)
 
         def store(g, t, single):
             if single:
@@ -303,21 +349,59 @@ def tile_groupqueryattention_pa_kernel(
                     in_=stage[g, t // 2][:].rearrange("p h t d -> p h (t d)"),
                 )
 
+        summed = {}
+
+        def tensor_add_first(g, t):
+            bank = psum.tile([P, HG, DH], F32, name="bank", tag="bank")
+            nc.tensor.matmul(
+                bank[:].rearrange("p h d -> p (h d)"),
+                lhsT=ident_f32[:],
+                rhs=prods[g, t][:, :, :, 0, :].rearrange("p h j e -> p (h j) e"),
+                start=True,
+                stop=False,
+            )
+            for j in range(2):
+                nc.tensor.matmul(
+                    bank[:, :, j * HALF : (j + 1) * HALF],
+                    lhsT=trig_t[:, j, t, :],
+                    rhs=fold[:, "qk".index(g[0]), j, :].unsqueeze(1).to_broadcast([P, HG, HALF]),
+                    start=False,
+                    stop=False,
+                )
+            summed[g, t] = bank
+
+        def tensor_add_second(g, t):
+            nc.tensor.matmul(
+                summed[g, t][:].rearrange("p h d -> p (h d)"),
+                lhsT=ident_f32[:],
+                rhs=prods[g, t][:, :, :, 1, :].rearrange("p h j e -> p (h j) e"),
+                start=False,
+                stop=True,
+            )
+
+        def empty_sum(g, t):
+            nc.scalar.copy(out=staged(g, t), in_=summed[g, t][:].rearrange("p h (j e) -> p h j e", j=2))
+            store(g, t, False)
+
         def empty_v(t):
             nc.scalar.copy(out=staged("v", t), in_=acc["v", t][:].rearrange("p h (j e) -> p h j e", j=2))
+            store("v", t, False)
 
         steps = []
-        q_left = [("q%d" % g, t) for g in range(4) for t in range(TILES)]
-        k_left = [("k", t) for t in range(TILES)]
-        for s in range(5 * TILES):
-            steps.append(k_left.pop(0) if (s >= 14 and s % 3 == 2 and k_left) else q_left.pop(0))
+        pair_end = []
+        k_next = 0
+        for n in range(16):
+            steps += [("q%d" % (n // 4), 2 * (n % 4)), ("q%d" % (n // 4), 2 * (n % 4) + 1)]
+            pair_end.append(len(steps) - 1)
+            if n in K_AFTER_PAIRS:
+                steps.append(("k", k_next))
+                k_next += 1
         n_steps = len(steps)
+        k_pool_tiles = list(range(TILES - N_TENSOR_ADDS))
+        tensor_steps = {("k", t) for t in range(TILES) if t not in k_pool_tiles}
+        pool_steps = {steps[pair_end[n]] for n in POOL_PAIRS} | {("k", t) for t in k_pool_tiles}
+        early = pair_end[3]
 
-        def pool_adds_both(s):
-            return s % 3 == 2 and s < n_steps - 3
-
-        turn_x(0)
-        empty_x(0)
         nc.tensor.matmul(
             spread[:].rearrange("p a d -> p (a d)"),
             lhsT=ones[:],
@@ -325,91 +409,123 @@ def tile_groupqueryattention_pa_kernel(
             start=True,
             stop=True,
         )
+        turn_x(0)
+        empty_x(0)
+        make_folds()
         make_gains("q")
-        make_diags()
         quant_x(0)
-        for b in range(2):
-            turn_w("q0", b)
-            empty_w("q0", b)
-        table_cos(nc.vector, "q", 0, TILES)
-        quant_w_bank("q0", 0)
-        quant_w_bank("q0", 1)
-        table_sin(nc.vector, "q", 0, TILES)
-        for b in range(2, 4):
+        arrange_trig()
+        make_table(nc.vector, "q", 0, 4)
+        for b in range(4):
             turn_w("q0", b)
             empty_w("q0", b)
             quant_w_bank("q0", b)
-        make_gains("k")
+            if b == 1:
+                make_table(nc.vector, "q", 4, 6)
         turn_x(1)
         empty_x(1)
-        turn_trig("cos", cos_sb)
-        nc.scalar.copy(out=cos_t[:], in_=turned["cos"][:])
+        turn_x(2)
+        empty_x(2)
+        turn_x(3)
+        empty_x(3, nc.vector.tensor_copy)
         project(*steps[0])
         quant_x(1)
-        turn_trig("sin", sin_sb)
-        for t0 in range(0, TILES, 2):
-            table_cos(nc.gpsimd, "k", t0, t0 + 2)
-            table_sin(nc.gpsimd, "k", t0, t0 + 2)
-        turn_x(2)
+        make_table(nc.vector, "q", 6, TILES)
+        quant_x(2, 2)
+        gain_part("k", DH, 2 * DH, 0, 1.0)
+        make_table(nc.gpsimd, "k", 0, 2)
+        make_table(nc.gpsimd, "k", 2, 4)
+        for j in range(2):
+            turn_trig(j)
         squares(*steps[0])
-        nc.scalar.copy(out=sin_t[:], in_=turned["sin"][:])
+        nc.scalar.copy(out=trig_t[:, 0], in_=turned["trig", 0][:])
         inverse_rms(*steps[0])
-        empty_x(2)
-        project(*steps[1])
-        quant_x(2)
-        rotate_shift("q", 0, shift_ps[0])
-        rotate_shift("q", 1, shift_ps[1])
-        turn_x(3)
+        nc.vector.tensor_copy(out=trig_t[:, 1], in_=turned["trig", 1][:])
+        for s in range(1, MX_AHEAD):
+            project(*steps[s])
+        turn_x(4)
+        turn_x(5)
+        shift_ps[0] = psum.tile([P, 2, 2, DH], F32, name="bank", tag="bank")
+        for t in range(TILES):
+            rotate_shift("q", t, shift_ps[t // 2 % 2][:, t // 4, t % 2, :])
 
-        turns = {0: [("x", 4)], 1: [("x", 5), ("q1", 0)], 2: [("x", 6), ("q1", 1)], 3: [("x", 7), ("q1", 2), ("q1", 3)]}
-        first_turn = {"k": 5, "q2": 10, "v": 14, "q3": 18}
-        for g, s0 in first_turn.items():
-            for b in range(4):
-                turns[s0 + b] = [(g, b)]
-        turns[-1] = [("x", 3)]
-        v_slot = {22 + 2 * t: t for t in range(TILES)}
+        turns = {-1: [("x", 4), ("x", 5)], 0: [("x", 6), ("x", 7)]}
+        quants = {pair_end[0]: ("x", 4), pair_end[1]: ("x", 6)}
+        late_quants = {}
+        for i, g in enumerate(W_ORDER[:2]):
+            turns[2 * i + 1] = [(g, 0), (g, 1)]
+            turns[2 * i + 2] = [(g, 2), (g, 3)]
+            quants[pair_end[i + 2]] = (g,)
+        for i, g in enumerate(W_ORDER[2:]):
+            s = pair_end[LATE_QUANTS[i]]
+            turns[LATE_TURNS[i]] = [(g, 0), (g, 1)]
+            turns[LATE_TURNS[i] + 2 - (i == 0)] = [(g, 2), (g, 3)]
+            late_quants.setdefault(s + 1, []).append(g)
+        v_slot = {V_FIRST + V_STEP * t: t for t in range(TILES)}
 
-        for s in range(n_steps + 1):
-            if s + 2 < n_steps:
-                project(*steps[s + 2])
+        for s in range(n_steps + 4):
+            if s + MX_AHEAD < n_steps:
+                project(*steps[s + MX_AHEAD])
             if s in v_slot:
                 project("v", v_slot[s])
+            if 0 <= s - LAG - 1 < n_steps and steps[s - LAG - 1] in tensor_steps:
+                tensor_add_second(*steps[s - LAG - 1])
+            if 0 <= s - LAG < n_steps and steps[s - LAG] in tensor_steps:
+                tensor_add_first(*steps[s - LAG])
             for g, b in turns.get(s, []):
                 if g == "x":
                     turn_x(b)
                 else:
                     turn_w(g, b)
-            if s in (9, 10):
-                rotate_shift_k(s - 9)
+            if s == 11 and k_pool_tiles:
+                shifts_for_pool("k", k_pool_tiles)
+            copies = []
+            for g, b in turns.get(s - 1, []):
+                copies.append((empty_x, b) if g == "x" else (empty_w, g, b))
+            for odd in range(2):
+                if s == pair_end[3 + 5 * odd] :
+                    dst = shift_sb["q"][:].rearrange("p (a b c) d -> p a b c d", a=2, b=2)[:, :, odd]
+                    copies.append((nc.scalar.copy, dst, shift_ps[odd][:]))
+            if s == 12 and k_pool_tiles:
+                copies.append((empty_shifts, "k", k_pool_tiles))
+            if s - 1 in v_slot:
+                copies.append((empty_v, v_slot[s - 1]))
+            if 0 <= s - LAG - 2 < n_steps and steps[s - LAG - 2] in tensor_steps:
+                copies.append((empty_sum,) + steps[s - LAG - 2])
             if s + 1 < n_steps:
                 squares(*steps[s + 1])
-            for g, b in turns.get(s - 1, []):
-                if g == "x":
-                    empty_x(b)
-                else:
-                    empty_w(g, b)
-            if s in (10, 11):
-                nc.scalar.copy(out=shift_sb["k"][:, 4 * (s - 10) : 4 * (s - 9), :], in_=turned["shift_k", s - 10][:])
-            if s - 1 in v_slot:
-                empty_v(v_slot[s - 1])
-                store("v", v_slot[s - 1], False)
+            for call in copies[:1]:
+                call[0](*call[1:])
             if s + 1 < n_steps:
                 inverse_rms(*steps[s + 1])
-            if s in (1, 3):
-                nc.scalar.copy(out=shift_sb["q"][:, 2 * (s - 1) : 2 * (s + 1), :], in_=shift_ps[(s - 1) // 2][:])
+            for call in copies[1:]:
+                call[0](*call[1:])
             if s < n_steps:
                 multiply(*steps[s])
-            for g, b in turns.get(s - 1, []):
-                if g == "x":
-                    quant_x(b)
-                elif b == 3:
-                    quant_w(g)
-            if s >= 1:
-                g, t = steps[s - 1]
-                last = s - 1 >= n_steps - 2
-                if pool_adds_both(s - 1):
-                    add_shift(nc.gpsimd, g, t, shift_sb[g[0]][:, t, :])
+            if s in quants:
+                if quants[s][0] == "x":
+                    quant_x(quants[s][1], 2)
                 else:
-                    add_shift(nc.vector, g, t, shift_ps[t // 4][:, t % 4, :])
-                add_second(nc.vector if s == n_steps else nc.gpsimd, g, t)
-                store(g, t, last)
+                    quant_w(quants[s][0])
+            for d in range(n_steps):
+                g, t = steps[d]
+                if d + (d > early) != s or (g, t) in tensor_steps:
+                    continue
+                if d >= n_steps - 2:
+                    add_last(g, t, shift_ps[1][:, t // 4, t % 2, :])
+                    if t % 2 == 1:
+                        add_last_second(g, t - 1)
+                        add_last_second(g, t)
+                elif t % 2 == 1:
+                    if (g, t) in pool_steps:
+                        add_shift(nc.gpsimd, g, t // 2, shift_sb[g[0]][:, t - 1 : t + 1, :])
+                    else:
+                        add_shift(nc.vector, g, t // 2, shift_ps[t // 2 % 2][:, t // 4])
+                    for w in late_quants.get(s, []):
+                        quant_w(w)
+                    add_second(nc.gpsimd, g, t // 2)
+                    store(g, t, False)
+            if s == pair_end[0]:
+                make_table(nc.gpsimd, "k", 4, 6)
+            if s == pair_end[1]:
+                make_table(nc.gpsimd, "k", 6, TILES)

@@ -19,21 +19,17 @@ ALU = mybir.AluOpType
 
 P = 128
 PASSES = 2
+PASS_WORDS = 256
 TILES = S // P
-HG = 4
-NCOL = HG * DH
-WORDS = 256
-N_TENSOR_ADDS = 8
-K_AFTER_PAIRS = (4, 6, 8, 9, 10, 11, 12, 13)
-POOL_PAIRS = (4, 6, 8, 10, 12, 13)
-PR_BUFS = 3
-W_ORDER = ("q1", "k", "q2", "v", "q3")
-V_FIRST = 19
-V_STEP = 2
-MX_AHEAD = 2
-LAG = 1
-LATE_TURNS = (5, 8, 14)
-LATE_QUANTS = (5, 7, 9)
+HEADS = 4
+NCOL = HEADS * DH
+W_BANKS = 4
+Q_GROUPS = ("q0", "q1", "q2", "q3")
+Q_PAIRS = len(Q_GROUPS) * TILES // 2
+EARLY_GROUPS = ("q0", "q1", "k")
+LATE_GROUPS = ("q2", "v", "q3")
+FIRST_LATE_PAIR = TILES // 2
+V_EVERY = 2
 
 
 def tile_groupqueryattention_pa_kernel(
@@ -47,21 +43,20 @@ def tile_groupqueryattention_pa_kernel(
         psum_keep = ctx.enter_context(tc.psum_pool(name="psum_keep", bufs=1))
         ctx.enter_context(tc.manual_schedule())
 
-        groups = ["q0", "q1", "q2", "q3", "k", "v"]
-        w_rows = {"q%d" % g: wq[g * NCOL : (g + 1) * NCOL, :] for g in range(4)}
+        w_rows = {g: wq[i * NCOL : (i + 1) * NCOL, :] for i, g in enumerate(Q_GROUPS)}
         w_rows["k"] = wk
         w_rows["v"] = wv
         out_q = out_0[0].rearrange("h (p t) d -> p h t d", t=TILES)
-        out_of = {"q%d" % g: out_q[:, g * HG : (g + 1) * HG] for g in range(4)}
+        out_of = {g: out_q[:, i * HEADS : (i + 1) * HEADS] for i, g in enumerate(Q_GROUPS)}
         out_of["k"] = out_1[0].rearrange("h (p t) d -> p h t d", t=TILES)
         out_of["v"] = out_2[0].rearrange("h (p t) d -> p h t d", t=TILES)
 
         x_raw = keep.tile([P, TILES, D], BF16, align_bytes=64)
-        w_raw = {g: keep.tile([P, HG, D], BF16, name="w_raw_" + g, align_bytes=64) for g in groups}
+        w_raw = {g: keep.tile([P, HEADS, D], BF16, name="w_raw_" + g, align_bytes=64) for g in w_rows}
         x_codes = keep.tile([P, TILES, PASSES, P], U32, align_bytes=64)
         x_scales = keep.tile([P, TILES, PASSES, P], U8, align_bytes=64)
-        w_codes = {g: keep.tile([P, PASSES, NCOL], U32, name="w_codes_" + g, align_bytes=64) for g in groups}
-        w_scales = {g: keep.tile([P, PASSES, NCOL], U8, name="w_scales_" + g, align_bytes=64) for g in groups}
+        w_codes = {g: keep.tile([P, PASSES, NCOL], U32, name="w_codes_" + g, align_bytes=64) for g in w_rows}
+        w_scales = {g: keep.tile([P, PASSES, NCOL], U8, name="w_scales_" + g, align_bytes=64) for g in w_rows}
         cos_sb = keep.tile([P, TILES, DH], BF16)
         sin_sb = keep.tile([P, TILES, DH], BF16)
         trig = keep.tile([P, TILES, 4, HALF], BF16)
@@ -70,12 +65,15 @@ def tile_groupqueryattention_pa_kernel(
         ones = keep.tile([P, P], BF16)
         ident_f32 = keep.tile([P, P], F32)
         ident_bf = keep.tile([P, P], BF16)
-        gain = {n: keep.tile([P, 2, DH], F32, name="gain_" + n) for n in "qk"}
+        gain = {n: keep.tile([P, 4 * HALF], F32, name="gain_" + n) for n in "qk"}
         diag = keep.tile([P, 2, DH], BF16)
         fold = keep.tile([P, 2, 2, HALF], BF16)
-        table = {n: keep.tile([P, TILES, 4, HALF], F32, name="table_" + n) for n in "qk"}
-        shift_sb = {n: keep.tile([P, TILES, DH], F32, name="shift_sb_" + n) for n in "q"}
-        shift_ps = {1: psum_keep.tile([P, 2, 2, DH], F32, name="shift_ps_odd")}
+        table = {n: keep.tile([P, TILES, 4 * HALF], F32, name="table_" + n) for n in "qk"}
+        shift_even_sb = keep.tile([P, 2, 2, DH], F32)
+        shift_ps = {1: psum_keep.tile([P, 2, 2, DH], F32, name="shift_odd_ps")}
+
+        def new_bank(shape, dtype=F32):
+            return psum.tile(shape, dtype, name="bank", tag="bank")
 
         nc.vector.memset(vec[:], 0.0)
         nc.vector.memset(ones[:], 1.0)
@@ -86,36 +84,38 @@ def tile_groupqueryattention_pa_kernel(
         def load_x(t0, t1):
             nc.sync.dma_start(out=x_raw[:, t0:t1, :], in_=x_view[:, t0:t1, :])
 
-        def load_w(g, j0, j1):
+        def load_w(g, h0, h1):
             nc.sync.dma_start(
-                out=w_raw[g][:, j0:j1, :], in_=w_rows[g].rearrange("(j p) k -> p j k", p=P)[:, j0:j1, :]
+                out=w_raw[g][:, h0:h1, :], in_=w_rows[g].rearrange("(h p) k -> p h k", p=P)[:, h0:h1, :]
             )
 
         load_x(0, 1)
         for i, row in enumerate((q_scale, q_shift, k_scale, k_shift)):
             nc.sync.dma_start(out=vec[0:1, i, :], in_=row.rearrange("(o d) -> o d", o=1))
         load_w("q0", 0, 2)
+        load_w("q0", 2, HEADS)
+        load_x(1, 2)
         nc.sync.dma_start(out=cos_sb[:], in_=cos_thetas.rearrange("(p t) d -> p t d", t=TILES))
         nc.sync.dma_start(out=sin_sb[:], in_=sin_thetas.rearrange("(p t) d -> p t d", t=TILES))
-        load_w("q0", 2, 4)
-        load_x(1, 2)
         load_x(2, 4)
-        load_x(4, 8)
-        for g in W_ORDER:
-            load_w(g, 0, HG)
+        load_x(4, TILES)
+        for g in EARLY_GROUPS[1:] + LATE_GROUPS:
+            load_w(g, 0, HEADS)
 
         turned = {}
         grouped = {}
 
+        def turn_words(dst, rows, c):
+            words = rows.bitcast(F32)
+            for u in range(2):
+                nc.tensor.transpose(
+                    dst[:, u, :], words[:, PASS_WORDS * c + u : PASS_WORDS * (c + 1) : 2], ident_f32[:]
+                )
+
         def turn_x(t):
-            bank = psum.tile([P, PASSES, 2, P], F32, name="bank", tag="bank")
-            words = x_raw[:, t, :].bitcast(F32)
+            turned["x", t] = new_bank([P, PASSES, 2, P])
             for c in range(PASSES):
-                for u in range(2):
-                    nc.tensor.transpose(
-                        bank[:, c, u, :], words[:, WORDS * c + u : WORDS * (c + 1) : 2], ident_f32[:]
-                    )
-            turned["x", t] = bank
+                turn_words(turned["x", t][:, c], x_raw[:, t, :], c)
 
         def empty_x(t, copy=nc.scalar.copy):
             if t % 2 == 0:
@@ -124,58 +124,54 @@ def tile_groupqueryattention_pa_kernel(
                 )
             copy(out=grouped["x", t // 2][:, t % 2], in_=turned["x", t][:].rearrange("p c u r -> p c r u"))
 
-        def quant_x(t, n=1):
+        def quant_x(t, count=1):
             nc.vector.quantize_mx(
-                out=x_codes[:, t : t + n].rearrange("p t c r -> p (t c r)").bitcast(E5M2X4),
-                scales=x_scales[:, t : t + n].rearrange("p t c r -> p (t c r)"),
-                in_=grouped["x", t // 2][:, t % 2 : t % 2 + n].rearrange("p t c r u -> p (t c r u)").bitcast(BF16),
+                out=x_codes[:, t : t + count].rearrange("p t c r -> p (t c r)").bitcast(E5M2X4),
+                scales=x_scales[:, t : t + count].rearrange("p t c r -> p (t c r)"),
+                in_=grouped["x", t // 2][:, t % 2 : t % 2 + count]
+                .rearrange("p t c r u -> p (t c r u)")
+                .bitcast(BF16),
             )
 
         def turn_w(g, b):
-            pair, c = divmod(b, PASSES)
-            bank = psum.tile([P, 2, 2, P], F32, name="bank", tag="bank")
+            h0, c = 2 * (b // PASSES), b % PASSES
+            turned[g, b] = new_bank([P, 2, 2, P])
             for j in range(2):
-                words = w_raw[g][:, 2 * pair + j, :].bitcast(F32)
-                for u in range(2):
-                    nc.tensor.transpose(
-                        bank[:, j, u, :], words[:, WORDS * c + u : WORDS * (c + 1) : 2], ident_f32[:]
-                    )
-            turned[g, b] = bank
+                turn_words(turned[g, b][:, j], w_raw[g][:, h0 + j, :], c)
 
         def empty_w(g, b):
-            pair, c = divmod(b, PASSES)
+            h0, c = 2 * (b // PASSES), b % PASSES
             if b == 0:
                 grouped[g] = work.tile(
-                    [P, PASSES, HG, P, 2], F32, name="w_grouped", tag="w_grouped", bufs=3, align_bytes=64
+                    [P, PASSES, HEADS, P, 2], F32, name="w_grouped", tag="w_grouped", bufs=3, align_bytes=64
                 )
             nc.scalar.copy(
-                out=grouped[g][:, c, 2 * pair : 2 * pair + 2],
-                in_=turned[g, b][:].rearrange("p j u r -> p j r u"),
+                out=grouped[g][:, c, h0 : h0 + 2], in_=turned[g, b][:].rearrange("p j u r -> p j r u")
             )
 
         def quant_w_bank(g, b):
-            pair, c = divmod(b, PASSES)
-            cols = slice(2 * pair * P, 2 * (pair + 1) * P)
+            h0, c = 2 * (b // PASSES), b % PASSES
+            cols = slice(h0 * P, (h0 + 2) * P)
             nc.vector.quantize_mx(
                 out=w_codes[g][:, c, cols].bitcast(E4M3X4),
                 scales=w_scales[g][:, c, cols],
-                in_=grouped[g][:, c, 2 * pair : 2 * pair + 2].rearrange("p j r u -> p (j r u)").bitcast(BF16),
+                in_=grouped[g][:, c, h0 : h0 + 2].rearrange("p j r u -> p (j r u)").bitcast(BF16),
             )
 
         def quant_w(g):
             nc.vector.quantize_mx(
                 out=w_codes[g][:].rearrange("p c n -> p (c n)").bitcast(E4M3X4),
                 scales=w_scales[g][:].rearrange("p c n -> p (c n)"),
-                in_=grouped[g][:].rearrange("p c j r u -> p (c j r u)").bitcast(BF16),
+                in_=grouped[g][:].rearrange("p c h r u -> p (c h r u)").bitcast(BF16),
             )
 
         acc = {}
 
         def project(g, t):
-            bank = psum.tile([P, HG, DH], F32, name="bank", tag="bank")
+            acc[g, t] = new_bank([P, HEADS, DH])
             for c in range(PASSES):
                 nc.tensor.matmul_mx(
-                    out=bank[:].rearrange("p h d -> p (h d)"),
+                    out=acc[g, t][:].rearrange("p h d -> p (h d)"),
                     lhsT=x_codes[:, t, c, :].bitcast(E5M2X4),
                     lhsT_scale=x_scales[:, t, c, :],
                     rhs=w_codes[g][:, c, :].bitcast(E4M3X4),
@@ -183,349 +179,377 @@ def tile_groupqueryattention_pa_kernel(
                     start=(c == 0),
                     stop=(c == PASSES - 1),
                 )
-            acc[g, t] = bank
 
-        spread = psum.tile([P, 4, DH], F32, name="bank", tag="bank")
+        spread = new_bank([P, 4, DH])
 
-        def gain_part(n, lo, hi, src, sign):
-            s = spread[:, 2 * "qk".index(n), :]
+        def spread_vectors():
+            nc.tensor.matmul(
+                spread[:].rearrange("p a d -> p (a d)"),
+                lhsT=ones[:],
+                rhs=vec[:].rearrange("p a d -> p (a d)"),
+                start=True,
+                stop=True,
+            )
+
+        def gain_part(n, cols, scale_cols, sign):
             nc.vector.tensor_scalar(
-                out=gain[n][:].rearrange("p j d -> p (j d)")[:, lo:hi],
-                in0=s[:, src : src + hi - lo],
+                out=gain[n][:, cols],
+                in0=spread[:, 2 * "qk".index(n), scale_cols],
                 scalar1=sign,
                 scalar2=sign,
                 op0=ALU.mult,
                 op1=ALU.add,
             )
 
-        def make_gains(n):
-            gain_part(n, 0, HALF, 0, 1.0)
-            gain_part(n, HALF, DH, HALF, -1.0)
-            gain_part(n, DH, 2 * DH, 0, 1.0)
+        def gain_out1(n):
+            gain_part(n, slice(0, HALF), slice(0, HALF), 1.0)
+            gain_part(n, slice(HALF, DH), slice(HALF, DH), -1.0)
 
-        def make_folds():
+        def gain_out2(n):
+            gain_part(n, slice(DH, 2 * DH), slice(0, DH), 1.0)
+
+        def make_diag():
             nc.vector.tensor_tensor(
                 out=diag[:],
                 in0=spread[:, 1:4:2, :],
                 in1=ident_bf[:].unsqueeze(1).to_broadcast([P, 2, DH]),
                 op=ALU.mult,
             )
-            gain_part("k", 0, HALF, 0, 1.0)
-            gain_part("k", HALF, DH, HALF, -1.0)
+
+        def make_folds():
             for j, op in enumerate((ALU.subtract, ALU.add)):
                 nc.vector.tensor_tensor(out=fold[:, :, j, :], in0=diag[:, :, :HALF], in1=diag[:, :, HALF:], op=op)
 
-        def arrange_trig():
-            nc.scalar.copy(out=trig[:, :, 0:4:3, :], in_=cos_sb[:].rearrange("p t (j e) -> p t j e", j=2))
-            nc.scalar.copy(out=trig[:, :, 1:3, :].rearrange("p t j e -> p t (j e)"), in_=sin_sb[:])
+        def arrange_cos():
+            nc.vector.tensor_copy(out=trig[:, :, 0:4:3, :], in_=cos_sb[:].rearrange("p t (j e) -> p t j e", j=2))
 
-        def make_table(engine, n, t0, t1):
+        def arrange_sin():
+            nc.vector.tensor_copy(out=trig[:, :, 1:3, :].rearrange("p t j e -> p t (j e)"), in_=sin_sb[:])
+
+        def make_table(engine, n, pair):
+            tiles = slice(2 * pair, 2 * pair + 2)
             engine.tensor_tensor(
-                out=table[n][:, t0:t1].rearrange("p t a e -> p t (a e)"),
-                in0=trig[:, t0:t1].rearrange("p t a e -> p t (a e)"),
-                in1=gain[n][:].rearrange("p j d -> p (j d)").unsqueeze(1).to_broadcast([P, t1 - t0, 2 * DH]),
+                out=table[n][:, tiles],
+                in0=trig[:, tiles].rearrange("p t a e -> p t (a e)"),
+                in1=gain[n][:].unsqueeze(1).to_broadcast([P, 2, 4 * HALF]),
                 op=ALU.mult,
             )
 
         def turn_trig(j):
-            bank = psum.tile([P, TILES, P], BF16, name="bank", tag="bank")
+            turned["trig", j] = new_bank([P, TILES, P], BF16)
             for t in range(TILES):
                 nc.tensor.transpose(
-                    bank[:, t, :], trig[:, t, 2 * j : 2 * j + 2, :].rearrange("p a e -> p (a e)"), ident_bf[:]
-                )
-            turned["trig", j] = bank
-
-        def rotate_shift(n, t, dst):
-            for j in range(2):
-                nc.tensor.matmul(
-                    dst[:, j * HALF : (j + 1) * HALF],
-                    lhsT=trig_t[:, j, t, :],
-                    rhs=fold[:, "qk".index(n), j, :],
-                    start=True,
-                    stop=True,
+                    turned["trig", j][:, t, :],
+                    trig[:, t, 2 * j : 2 * j + 2, :].rearrange("p a e -> p (a e)"),
+                    ident_bf[:],
                 )
 
-        def shifts_for_pool(n, tiles):
-            bank = psum.tile([P, 4, DH], F32, name="bank", tag="bank")
-            for i, t in enumerate(tiles):
-                rotate_shift(n, t, bank[:, i, :])
-            turned["shift", n] = bank
+        def empty_trig(j, copy):
+            copy(out=trig_t[:, j], in_=turned["trig", j][:])
 
-        def empty_shifts(n, tiles):
-            for i, t in enumerate(tiles):
-                if i % 2 == 0:
-                    w = min(2, len(tiles) - i)
-                    nc.scalar.copy(out=shift_sb[n][:, t : t + w, :], in_=turned["shift", n][:, i : i + w, :])
+        def rotate_q_shifts():
+            shift_ps[0] = new_bank([P, 2, 2, DH])
+            for t in range(TILES):
+                for j in range(2):
+                    nc.tensor.matmul(
+                        shift_ps[t // 2 % 2][:, t // 4, t % 2, j * HALF : (j + 1) * HALF],
+                        lhsT=trig_t[:, j, t, :],
+                        rhs=fold[:, 0, j, :],
+                        start=True,
+                        stop=True,
+                    )
 
+        def empty_even_shifts():
+            nc.scalar.copy(out=shift_even_sb[:], in_=shift_ps[0][:])
+
+        squared = {}
         sums = {}
         rstd = {}
-        prods = {}
+        pair_products = {}
+        tile_products = {}
+        summed = {}
         stage = {}
 
-        def squares(g, t):
-            junk = work.tile([P, HG, DH], BF16, name="junk", tag="junk", bufs=2)
-            ss = work.tile([P, HG], F32, name="ss", tag="ss", bufs=4)
-            for h in range(HG):
+        def squares(g, t, h0=0, h1=HEADS):
+            if h0 == 0:
+                squared[g, t] = work.tile([P, HEADS, DH], BF16, name="squared", tag="squared", bufs=2)
+                sums[g, t] = work.tile([P, HEADS], F32, name="sums", tag="sums", bufs=4)
+            for h in range(h0, h1):
                 nc.scalar.activation(
-                    out=junk[:, h, :], in_=acc[g, t][:, h, :], func=ACT.Square, accum_out=ss[:, h : h + 1]
+                    out=squared[g, t][:, h, :],
+                    in_=acc[g, t][:, h, :],
+                    func=ACT.Square,
+                    accum_out=sums[g, t][:, h : h + 1],
                 )
-            sums[g, t] = ss
 
         def inverse_rms(g, t):
-            r = work.tile([P, HG], F32, name="r", tag="r", bufs=4)
+            rstd[g, t] = work.tile([P, HEADS], F32, name="rstd", tag="rstd", bufs=4)
             nc.scalar.activation(
-                out=r[:], in_=sums[g, t][:], func=ACT.Abs_reciprocal_sqrt, scale=1.0 / DH, bias=EPS
+                out=rstd[g, t][:], in_=sums[g, t][:], func=ACT.Abs_reciprocal_sqrt, scale=1.0 / DH, bias=EPS
             )
-            rstd[g, t] = r
 
         def multiply(g, t):
             if (g, t) in tensor_steps:
-                prods[g, t] = work.tile([P, HG, 2, 2, HALF], F32, name="pr_one", tag="pr_one", bufs=2)
-                pr = prods[g, t][:]
+                tile_products[g, t] = work.tile(
+                    [P, HEADS, 2, 2, HALF], F32, name="tile_products", tag="tile_products", bufs=3
+                )
+                products = tile_products[g, t][:]
             else:
                 if t % 2 == 0:
-                    prods[g, t // 2] = work.tile([P, HG, 2, 2, 2, HALF], F32, name="pr", tag="pr", bufs=PR_BUFS)
-                pr = prods[g, t // 2][:, :, t % 2]
-            for h in range(HG):
+                    pair_products[g, t // 2] = work.tile(
+                        [P, HEADS, 2, 2, 2, HALF], F32, name="pair_products", tag="pair_products", bufs=3
+                    )
+                products = pair_products[g, t // 2][:, :, t % 2]
+            for h in range(HEADS):
                 nc.vector.scalar_tensor_tensor(
-                    out=pr[:, h].rearrange("p j s e -> p j (s e)"),
+                    out=products[:, h].rearrange("p j s e -> p j (s e)"),
                     in0=acc[g, t][:, h, :].unsqueeze(1).to_broadcast([P, 2, DH]),
                     scalar=rstd[g, t][:, h : h + 1],
-                    in1=table[g[0]][:, t].rearrange("p (j s) e -> p j (s e)", j=2),
+                    in1=table[g[0]][:, t].rearrange("p (j d) -> p j d", j=2),
                     op0=ALU.mult,
                     op1=ALU.mult,
                 )
 
-        def staged(g, t):
-            if t % 2 == 0:
-                stage[g, t // 2] = work.tile([P, HG, 2, DH], F32, name="stage", tag="stage", bufs=5)
-            return staged_view(g, t)
+        def new_stage(g, pair):
+            stage[g, pair] = work.tile([P, HEADS, 2, DH], F32, name="stage", tag="stage", bufs=5)
 
-        def staged_view(g, t):
+        def staged_tile(g, t):
             return stage[g, t // 2][:, :, t % 2, :].rearrange("p h (j e) -> p h j e", j=2)
 
-        def add_shift(engine, g, pair, shift):
-            stage[g, pair] = work.tile([P, HG, 2, DH], F32, name="stage", tag="stage", bufs=5)
+        def store_pair(g, pair):
+            nc.sync.dma_start(
+                out=out_of[g][:, :, 2 * pair : 2 * pair + 2, :].rearrange("p h t d -> p h (t d)"),
+                in_=stage[g, pair][:].rearrange("p h t d -> p h (t d)"),
+            )
+
+        def store_tile(g, t):
+            nc.sync.dma_start(out=out_of[g][:, :, t, :], in_=stage[g, t // 2][:, :, t % 2, :])
+
+        def add_shift(g, pair, on_gpsimd):
+            engine = nc.gpsimd if on_gpsimd else nc.vector
+            shift = shift_even_sb[:, pair // 2] if on_gpsimd else shift_ps[pair % 2][:, pair // 2]
+            new_stage(g, pair)
             engine.tensor_tensor(
                 out=stage[g, pair][:].rearrange("p h t (j e) -> p h (t j) e", j=2),
-                in0=prods[g, pair][:, :, :, :, 0, :].rearrange("p h t j e -> p h (t j) e"),
-                in1=shift.rearrange("p t (j e) -> p (t j) e", j=2).unsqueeze(1).to_broadcast([P, HG, 4, HALF]),
+                in0=pair_products[g, pair][:, :, :, :, 0, :].rearrange("p h t j e -> p h (t j) e"),
+                in1=shift.rearrange("p t (j e) -> p (t j) e", j=2).unsqueeze(1).to_broadcast([P, HEADS, 4, HALF]),
                 op=ALU.add,
             )
 
-        def add_second(engine, g, pair):
+        def add_second(g, pair):
             both = stage[g, pair][:].rearrange("p h t (j e) -> p (h t j) e", j=2)
-            engine.tensor_tensor(
+            nc.gpsimd.tensor_tensor(
                 out=both,
                 in0=both,
-                in1=prods[g, pair][:, :, :, :, 1, :].rearrange("p h t j e -> p (h t j) e"),
+                in1=pair_products[g, pair][:, :, :, :, 1, :].rearrange("p h t j e -> p (h t j) e"),
                 op=ALU.add,
             )
+            store_pair(g, pair)
 
-        def add_last(g, t, shift):
+        def finish_last_pair_tile(g, t):
             if t % 2 == 0:
-                stage[g, t // 2] = work.tile([P, HG, 2, DH], F32, name="stage", tag="stage", bufs=5)
-            pr = prods[g, t // 2][:, :, t % 2]
+                new_stage(g, t // 2)
+            products = pair_products[g, t // 2][:, :, t % 2]
+            shift = shift_ps[1][:, t // 4, t % 2, :].rearrange("p (j e) -> p j e", j=2)
             nc.vector.tensor_tensor(
-                out=staged_view(g, t),
-                in0=pr[:, :, :, 0, :],
-                in1=shift.rearrange("p (j e) -> p j e", j=2).unsqueeze(1).to_broadcast([P, HG, 2, HALF]),
+                out=staged_tile(g, t),
+                in0=products[:, :, :, 0, :],
+                in1=shift.unsqueeze(1).to_broadcast([P, HEADS, 2, HALF]),
                 op=ALU.add,
             )
-
-        def add_last_second(g, t):
-            pr = prods[g, t // 2][:, :, t % 2]
-            nc.vector.tensor_tensor(
-                out=staged_view(g, t), in0=staged_view(g, t), in1=pr[:, :, :, 1, :], op=ALU.add
+            engine = nc.vector if t % 2 else nc.gpsimd
+            engine.tensor_tensor(
+                out=staged_tile(g, t), in0=staged_tile(g, t), in1=products[:, :, :, 1, :], op=ALU.add
             )
-            store(g, t, True)
+            store_tile(g, t)
 
-        def store(g, t, single):
-            if single:
-                nc.sync.dma_start(out=out_of[g][:, :, t, :], in_=stage[g, t // 2][:, :, t % 2, :])
-            elif t % 2 == 1:
-                nc.sync.dma_start(
-                    out=out_of[g][:, :, t - 1 : t + 1, :].rearrange("p h t d -> p h (t d)"),
-                    in_=stage[g, t // 2][:].rearrange("p h t d -> p h (t d)"),
-                )
-
-        summed = {}
-
-        def tensor_add_first(g, t):
-            bank = psum.tile([P, HG, DH], F32, name="bank", tag="bank")
-            nc.tensor.matmul(
-                bank[:].rearrange("p h d -> p (h d)"),
-                lhsT=ident_f32[:],
-                rhs=prods[g, t][:, :, :, 0, :].rearrange("p h j e -> p (h j) e"),
-                start=True,
-                stop=False,
-            )
-            for j in range(2):
-                nc.tensor.matmul(
-                    bank[:, :, j * HALF : (j + 1) * HALF],
-                    lhsT=trig_t[:, j, t, :],
-                    rhs=fold[:, "qk".index(g[0]), j, :].unsqueeze(1).to_broadcast([P, HG, HALF]),
-                    start=False,
-                    stop=False,
-                )
-            summed[g, t] = bank
-
-        def tensor_add_second(g, t):
+        def tensor_add_products(g, t, s):
             nc.tensor.matmul(
                 summed[g, t][:].rearrange("p h d -> p (h d)"),
                 lhsT=ident_f32[:],
-                rhs=prods[g, t][:, :, :, 1, :].rearrange("p h j e -> p (h j) e"),
-                start=False,
-                stop=True,
+                rhs=tile_products[g, t][:, :, :, s, :].rearrange("p h j e -> p (h j) e"),
+                start=(s == 0),
+                stop=(s == 1),
             )
 
-        def empty_sum(g, t):
-            nc.scalar.copy(out=staged(g, t), in_=summed[g, t][:].rearrange("p h (j e) -> p h j e", j=2))
-            store(g, t, False)
+        def tensor_add_first(g, t):
+            summed[g, t] = new_bank([P, HEADS, DH])
+            tensor_add_products(g, t, 0)
+            for j in range(2):
+                nc.tensor.matmul(
+                    summed[g, t][:, :, j * HALF : (j + 1) * HALF],
+                    lhsT=trig_t[:, j, t, :],
+                    rhs=fold[:, "qk".index(g[0]), j, :].unsqueeze(1).to_broadcast([P, HEADS, HALF]),
+                    start=False,
+                    stop=False,
+                )
 
-        def empty_v(t):
-            nc.scalar.copy(out=staged("v", t), in_=acc["v", t][:].rearrange("p h (j e) -> p h j e", j=2))
-            store("v", t, False)
+        def empty_result(bank, g, t):
+            if t % 2 == 0:
+                new_stage(g, t // 2)
+            nc.scalar.copy(out=staged_tile(g, t), in_=bank[:].rearrange("p h (j e) -> p h j e", j=2))
+            if g in Q_GROUPS:
+                store_tile(g, t)
+            elif t % 2 == 1:
+                store_pair(g, t // 2)
 
+        quant_pairs = {FIRST_LATE_PAIR + 2 * i + 1: g for i, g in enumerate(LATE_GROUPS)}
         steps = []
         pair_end = []
-        k_next = 0
-        for n in range(16):
-            steps += [("q%d" % (n // 4), 2 * (n % 4)), ("q%d" % (n // 4), 2 * (n % 4) + 1)]
+        k_tiles = list(range(TILES))
+        for n in range(Q_PAIRS):
+            g, pair = Q_GROUPS[n // (TILES // 2)], n % (TILES // 2)
+            steps += [(g, 2 * pair), (g, 2 * pair + 1)]
             pair_end.append(len(steps) - 1)
-            if n in K_AFTER_PAIRS:
-                steps.append(("k", k_next))
-                k_next += 1
+            if k_tiles and n >= FIRST_LATE_PAIR and (n % 2 == 0 or n >= max(quant_pairs)):
+                steps.append(("k", k_tiles.pop(0)))
         n_steps = len(steps)
-        k_pool_tiles = list(range(TILES - N_TENSOR_ADDS))
-        tensor_steps = {("k", t) for t in range(TILES) if t not in k_pool_tiles}
-        pool_steps = {steps[pair_end[n]] for n in POOL_PAIRS} | {("k", t) for t in k_pool_tiles}
-        early = pair_end[3]
+        tensor_steps = {("k", t) for t in range(TILES)} | set(steps[n_steps - 4 : n_steps - 2])
 
-        nc.tensor.matmul(
-            spread[:].rearrange("p a d -> p (a d)"),
-            lhsT=ones[:],
-            rhs=vec[:].rearrange("p a d -> p (a d)"),
-            start=True,
-            stop=True,
-        )
         turn_x(0)
         empty_x(0)
+        spread_vectors()
+        make_diag()
+        gain_out1("q")
+        gain_out2("q")
         make_folds()
-        make_gains("q")
         quant_x(0)
-        arrange_trig()
-        make_table(nc.vector, "q", 0, 4)
-        for b in range(4):
+        gain_out1("k")
+        for b in range(W_BANKS):
             turn_w("q0", b)
             empty_w("q0", b)
-            quant_w_bank("q0", b)
-            if b == 1:
-                make_table(nc.vector, "q", 4, 6)
         turn_x(1)
         empty_x(1)
-        turn_x(2)
-        empty_x(2)
-        turn_x(3)
-        empty_x(3, nc.vector.tensor_copy)
-        project(*steps[0])
+        quant_w_bank("q0", 0)
+        quant_w_bank("q0", 1)
+        arrange_cos()
+        quant_w_bank("q0", 2)
+        arrange_sin()
+        quant_w_bank("q0", 3)
+        project("q0", 0)
         quant_x(1)
-        make_table(nc.vector, "q", 6, TILES)
-        quant_x(2, 2)
-        gain_part("k", DH, 2 * DH, 0, 1.0)
-        make_table(nc.gpsimd, "k", 0, 2)
-        make_table(nc.gpsimd, "k", 2, 4)
-        for j in range(2):
-            turn_trig(j)
-        squares(*steps[0])
-        nc.scalar.copy(out=trig_t[:, 0], in_=turned["trig", 0][:])
-        inverse_rms(*steps[0])
-        nc.vector.tensor_copy(out=trig_t[:, 1], in_=turned["trig", 1][:])
-        for s in range(1, MX_AHEAD):
-            project(*steps[s])
+        make_table(nc.vector, "q", 0)
+        turn_x(2)
+        project("q0", 1)
+        turn_x(3)
+        make_table(nc.vector, "q", 1)
+        empty_x(2, nc.vector.tensor_copy)
+        quant_x(2)
+        gain_out2("k")
+        for n, pair in (("k", 0), ("q", 2), ("q", 3), ("k", 1), ("k", 2)):
+            make_table(nc.gpsimd, n, pair)
+        project("q0", 2)
         turn_x(4)
         turn_x(5)
-        shift_ps[0] = psum.tile([P, 2, 2, DH], F32, name="bank", tag="bank")
-        for t in range(TILES):
-            rotate_shift("q", t, shift_ps[t // 2 % 2][:, t // 4, t % 2, :])
+        turn_trig(0)
+        turn_trig(1)
+        squares("q0", 0)
+        squares("q0", 1, 0, 1)
+        inverse_rms("q0", 0)
+        squares("q0", 1, 1, HEADS)
+        empty_x(3)
+        inverse_rms("q0", 1)
+        squares("q0", 2)
+        empty_x(4)
+        inverse_rms("q0", 2)
+        empty_x(5)
+        multiply("q0", 0)
+        multiply("q0", 1)
+        quant_x(3)
+        project("q0", 3)
+        turn_x(6)
+        turn_x(7)
+        multiply("q0", 2)
+        quant_x(4, 2)
+        empty_trig(0, nc.vector.tensor_copy)
+        project("q0", 4)
+        squares("q0", 3)
+        empty_trig(1, nc.scalar.copy)
+        inverse_rms("q0", 3)
+        empty_x(6)
+        empty_x(7)
+        rotate_q_shifts()
+        project("q0", 5)
+        multiply("q0", 3)
+        quant_x(6, 2)
+        for pair in range(2):
+            add_shift("q0", pair, False)
+            add_second("q0", pair)
+        for b in (0, 2):
+            t = 4 + b // 2
+            turn_w("q1", b)
+            turn_w("q1", b + 1)
+            project("q0", t + 2)
+            squares("q0", t)
+            empty_w("q1", b)
+            inverse_rms("q0", t)
+            empty_w("q1", b + 1)
+            multiply("q0", t)
+        add_shift("q0", 2, False)
+        quant_w("q1")
+        add_second("q0", 2)
+        make_table(nc.gpsimd, "k", 3)
+        for b in range(W_BANKS):
+            turn_w("k", b)
+        for t in (6, 7):
+            b = 2 * (t - 6)
+            squares("q0", t)
+            empty_w("k", b)
+            inverse_rms("q0", t)
+            empty_w("k", b + 1)
+            project(*steps[t + 2])
+            multiply("q0", t)
+        squares(*steps[TILES])
+        empty_even_shifts()
+        inverse_rms(*steps[TILES])
+        squares(*steps[TILES + 1])
+        quant_w("k")
+        add_shift("q0", 3, False)
+        add_second("q0", 3)
 
-        turns = {-1: [("x", 4), ("x", 5)], 0: [("x", 6), ("x", 7)]}
-        quants = {pair_end[0]: ("x", 4), pair_end[1]: ("x", 6)}
-        late_quants = {}
-        for i, g in enumerate(W_ORDER[:2]):
-            turns[2 * i + 1] = [(g, 0), (g, 1)]
-            turns[2 * i + 2] = [(g, 2), (g, 3)]
-            quants[pair_end[i + 2]] = (g,)
-        for i, g in enumerate(W_ORDER[2:]):
-            s = pair_end[LATE_QUANTS[i]]
-            turns[LATE_TURNS[i]] = [(g, 0), (g, 1)]
-            turns[LATE_TURNS[i] + 2 - (i == 0)] = [(g, 2), (g, 3)]
-            late_quants.setdefault(s + 1, []).append(g)
-        v_slot = {V_FIRST + V_STEP * t: t for t in range(TILES)}
+        late_banks = [(g, b) for g in LATE_GROUPS for b in range(W_BANKS)]
+        turns = {TILES - 1 + i: late_banks[i : i + 2] for i in range(0, len(late_banks), 2)}
+        quant_after = {pair_end[n]: g for n, g in quant_pairs.items()}
+        v_ready = [s for s, g in quant_after.items() if g == "v"][0] + 2
+        v_at = {v_ready + V_EVERY * t: t for t in range(TILES)}
+        for g, b in turns.pop(TILES - 1):
+            turn_w(g, b)
+            empty_w(g, b)
+        project(*steps[TILES + 2])
 
-        for s in range(n_steps + 4):
-            if s + MX_AHEAD < n_steps:
-                project(*steps[s + MX_AHEAD])
-            if s in v_slot:
-                project("v", v_slot[s])
-            if 0 <= s - LAG - 1 < n_steps and steps[s - LAG - 1] in tensor_steps:
-                tensor_add_second(*steps[s - LAG - 1])
-            if 0 <= s - LAG < n_steps and steps[s - LAG] in tensor_steps:
-                tensor_add_first(*steps[s - LAG])
+        def step_at(s):
+            return steps[s] if s < n_steps else None
+
+        for s in range(TILES, n_steps + 1):
+            if step_at(s + 3):
+                project(*steps[s + 3])
+            if s in v_at:
+                project("v", v_at[s])
+            if steps[s - 2] in tensor_steps:
+                tensor_add_products(*steps[s - 2], 1)
+            if steps[s - 1] in tensor_steps:
+                tensor_add_first(*steps[s - 1])
             for g, b in turns.get(s, []):
-                if g == "x":
-                    turn_x(b)
-                else:
-                    turn_w(g, b)
-            if s == 11 and k_pool_tiles:
-                shifts_for_pool("k", k_pool_tiles)
-            copies = []
-            for g, b in turns.get(s - 1, []):
-                copies.append((empty_x, b) if g == "x" else (empty_w, g, b))
-            for odd in range(2):
-                if s == pair_end[3 + 5 * odd] :
-                    dst = shift_sb["q"][:].rearrange("p (a b c) d -> p a b c d", a=2, b=2)[:, :, odd]
-                    copies.append((nc.scalar.copy, dst, shift_ps[odd][:]))
-            if s == 12 and k_pool_tiles:
-                copies.append((empty_shifts, "k", k_pool_tiles))
-            if s - 1 in v_slot:
-                copies.append((empty_v, v_slot[s - 1]))
-            if 0 <= s - LAG - 2 < n_steps and steps[s - LAG - 2] in tensor_steps:
-                copies.append((empty_sum,) + steps[s - LAG - 2])
-            if s + 1 < n_steps:
-                squares(*steps[s + 1])
-            for call in copies[:1]:
-                call[0](*call[1:])
-            if s + 1 < n_steps:
+                turn_w(g, b)
+            if step_at(s + 2):
+                squares(*steps[s + 2], 0, 1)
+            if step_at(s + 1):
                 inverse_rms(*steps[s + 1])
-            for call in copies[1:]:
-                call[0](*call[1:])
-            if s < n_steps:
+            if step_at(s + 2):
+                squares(*steps[s + 2], 1, HEADS)
+            for g, b in turns.get(s - 1, []):
+                empty_w(g, b)
+            if s - 1 in v_at:
+                empty_result(acc["v", v_at[s - 1]], "v", v_at[s - 1])
+            if steps[s - 3] in tensor_steps:
+                empty_result(summed[steps[s - 3]], *steps[s - 3])
+            if step_at(s):
                 multiply(*steps[s])
-            if s in quants:
-                if quants[s][0] == "x":
-                    quant_x(quants[s][1], 2)
-                else:
-                    quant_w(quants[s][0])
-            for d in range(n_steps):
-                g, t = steps[d]
-                if d + (d > early) != s or (g, t) in tensor_steps:
-                    continue
-                if d >= n_steps - 2:
-                    add_last(g, t, shift_ps[1][:, t // 4, t % 2, :])
-                    if t % 2 == 1:
-                        add_last_second(g, t - 1)
-                        add_last_second(g, t)
-                elif t % 2 == 1:
-                    if (g, t) in pool_steps:
-                        add_shift(nc.gpsimd, g, t // 2, shift_sb[g[0]][:, t - 1 : t + 1, :])
-                    else:
-                        add_shift(nc.vector, g, t // 2, shift_ps[t // 2 % 2][:, t // 4])
-                    for w in late_quants.get(s, []):
-                        quant_w(w)
-                    add_second(nc.gpsimd, g, t // 2)
-                    store(g, t, False)
-            if s == pair_end[0]:
-                make_table(nc.gpsimd, "k", 4, 6)
-            if s == pair_end[1]:
-                make_table(nc.gpsimd, "k", 6, TILES)
+            if n_steps - 2 <= s < n_steps:
+                finish_last_pair_tile(*steps[s])
+            if s - 1 in pair_end[FIRST_LATE_PAIR : Q_PAIRS - 2]:
+                g, pair = steps[s - 1][0], steps[s - 1][1] // 2
+                add_shift(g, pair, pair % 2 == 0)
+                if s - 1 in quant_after:
+                    quant_w(quant_after[s - 1])
+                add_second(g, pair)

from contextlib import ExitStack

import concourse.mybir as mybir
from concourse.masks import make_identity

S, D, H, KV, DH = 1024, 1024, 16, 4, 128
HALF = DH // 2
EPS = 1e-6
FLOPS = 2 * S * D * (H + 2 * KV) * DH

F32 = mybir.dt.float32
BF16 = mybir.dt.bfloat16
U32 = mybir.dt.uint32
U8 = mybir.dt.uint8
E5M2X4 = mybir.dt.float8_e5m2_x4
E4M3X4 = mybir.dt.float8_e4m3fn_x4
ACT = mybir.ActivationFunctionType
ALU = mybir.AluOpType

P = 128
PASSES = 2
PASS_WORDS = 256
TILES = S // P
HEADS = 4
NCOL = HEADS * DH
W_BANKS = 4
Q_GROUPS = ("q0", "q1", "q2", "q3")
Q_PAIRS = len(Q_GROUPS) * TILES // 2
EARLY_GROUPS = ("q0", "q1", "k")
LATE_GROUPS = ("q2", "v", "q3")
FIRST_LATE_PAIR = TILES // 2
V_EVERY = 2


def tile_groupqueryattention_pa_kernel(
    tc, x, sin_thetas, cos_thetas, wq, wk, wv, q_scale, q_shift, k_scale, k_shift, out_0, out_1, out_2
):
    nc = tc.nc
    with ExitStack() as ctx:
        keep = ctx.enter_context(tc.tile_pool(name="keep", bufs=1))
        work = ctx.enter_context(tc.tile_pool(name="work", bufs=2))
        psum = ctx.enter_context(tc.psum_pool(name="psum", bufs=7))
        psum_keep = ctx.enter_context(tc.psum_pool(name="psum_keep", bufs=1))
        ctx.enter_context(tc.manual_schedule())

        w_rows = {g: wq[i * NCOL : (i + 1) * NCOL, :] for i, g in enumerate(Q_GROUPS)}
        w_rows["k"] = wk
        w_rows["v"] = wv
        out_q = out_0[0].rearrange("h (p t) d -> p h t d", t=TILES)
        out_of = {g: out_q[:, i * HEADS : (i + 1) * HEADS] for i, g in enumerate(Q_GROUPS)}
        out_of["k"] = out_1[0].rearrange("h (p t) d -> p h t d", t=TILES)
        out_of["v"] = out_2[0].rearrange("h (p t) d -> p h t d", t=TILES)

        x_raw = keep.tile([P, TILES, D], BF16, align_bytes=64)
        w_raw = {g: keep.tile([P, HEADS, D], BF16, name="w_raw_" + g, align_bytes=64) for g in w_rows}
        x_codes = keep.tile([P, TILES, PASSES, P], U32, align_bytes=64)
        x_scales = keep.tile([P, TILES, PASSES, P], U8, align_bytes=64)
        w_codes = {g: keep.tile([P, PASSES, NCOL], U32, name="w_codes_" + g, align_bytes=64) for g in w_rows}
        w_scales = {g: keep.tile([P, PASSES, NCOL], U8, name="w_scales_" + g, align_bytes=64) for g in w_rows}
        cos_sb = keep.tile([P, TILES, DH], BF16)
        sin_sb = keep.tile([P, TILES, DH], BF16)
        trig = keep.tile([P, TILES, 4, HALF], BF16)
        trig_t = keep.tile([P, 2, TILES, P], BF16)
        vec = keep.tile([P, 4, DH], BF16)
        ones = keep.tile([P, P], BF16)
        ident_f32 = keep.tile([P, P], F32)
        ident_bf = keep.tile([P, P], BF16)
        gain = {n: keep.tile([P, 4 * HALF], F32, name="gain_" + n) for n in "qk"}
        diag = keep.tile([P, 2, DH], BF16)
        fold = keep.tile([P, 2, 2, HALF], BF16)
        table = {n: keep.tile([P, TILES, 4 * HALF], F32, name="table_" + n) for n in "qk"}
        shift_even_sb = keep.tile([P, 2, 2, DH], F32)
        shift_ps = {1: psum_keep.tile([P, 2, 2, DH], F32, name="shift_odd_ps")}

        def new_bank(shape, dtype=F32):
            return psum.tile(shape, dtype, name="bank", tag="bank")

        nc.vector.memset(vec[:], 0.0)
        nc.vector.memset(ones[:], 1.0)
        make_identity(nc, ident_f32[:])
        make_identity(nc, ident_bf[:])
        x_view = x[0].rearrange("(p t) k -> p t k", t=TILES)

        def load_x(t0, t1):
            nc.sync.dma_start(out=x_raw[:, t0:t1, :], in_=x_view[:, t0:t1, :])

        def load_w(g, h0, h1):
            nc.sync.dma_start(
                out=w_raw[g][:, h0:h1, :], in_=w_rows[g].rearrange("(h p) k -> p h k", p=P)[:, h0:h1, :]
            )

        load_x(0, 1)
        for i, row in enumerate((q_scale, q_shift, k_scale, k_shift)):
            nc.sync.dma_start(out=vec[0:1, i, :], in_=row.rearrange("(o d) -> o d", o=1))
        load_w("q0", 0, 2)
        load_w("q0", 2, HEADS)
        load_x(1, 2)
        nc.sync.dma_start(out=cos_sb[:], in_=cos_thetas.rearrange("(p t) d -> p t d", t=TILES))
        nc.sync.dma_start(out=sin_sb[:], in_=sin_thetas.rearrange("(p t) d -> p t d", t=TILES))
        load_x(2, 4)
        load_x(4, TILES)
        for g in EARLY_GROUPS[1:] + LATE_GROUPS:
            load_w(g, 0, HEADS)

        turned = {}
        grouped = {}

        def turn_words(dst, rows, c):
            words = rows.bitcast(F32)
            for u in range(2):
                nc.tensor.transpose(
                    dst[:, u, :], words[:, PASS_WORDS * c + u : PASS_WORDS * (c + 1) : 2], ident_f32[:]
                )

        def turn_x(t):
            turned["x", t] = new_bank([P, PASSES, 2, P])
            for c in range(PASSES):
                turn_words(turned["x", t][:, c], x_raw[:, t, :], c)

        def empty_x(t, copy=nc.scalar.copy):
            if t % 2 == 0:
                grouped["x", t // 2] = work.tile(
                    [P, 2, PASSES, P, 2], F32, name="x_grouped", tag="x_grouped", bufs=2, align_bytes=64
                )
            copy(out=grouped["x", t // 2][:, t % 2], in_=turned["x", t][:].rearrange("p c u r -> p c r u"))

        def quant_x(t, count=1):
            nc.vector.quantize_mx(
                out=x_codes[:, t : t + count].rearrange("p t c r -> p (t c r)").bitcast(E5M2X4),
                scales=x_scales[:, t : t + count].rearrange("p t c r -> p (t c r)"),
                in_=grouped["x", t // 2][:, t % 2 : t % 2 + count]
                .rearrange("p t c r u -> p (t c r u)")
                .bitcast(BF16),
            )

        def turn_w(g, b):
            h0, c = 2 * (b // PASSES), b % PASSES
            turned[g, b] = new_bank([P, 2, 2, P])
            for j in range(2):
                turn_words(turned[g, b][:, j], w_raw[g][:, h0 + j, :], c)

        def empty_w(g, b):
            h0, c = 2 * (b // PASSES), b % PASSES
            if b == 0:
                grouped[g] = work.tile(
                    [P, PASSES, HEADS, P, 2], F32, name="w_grouped", tag="w_grouped", bufs=3, align_bytes=64
                )
            nc.scalar.copy(
                out=grouped[g][:, c, h0 : h0 + 2], in_=turned[g, b][:].rearrange("p j u r -> p j r u")
            )

        def quant_w_bank(g, b):
            h0, c = 2 * (b // PASSES), b % PASSES
            cols = slice(h0 * P, (h0 + 2) * P)
            nc.vector.quantize_mx(
                out=w_codes[g][:, c, cols].bitcast(E4M3X4),
                scales=w_scales[g][:, c, cols],
                in_=grouped[g][:, c, h0 : h0 + 2].rearrange("p j r u -> p (j r u)").bitcast(BF16),
            )

        def quant_w(g):
            nc.vector.quantize_mx(
                out=w_codes[g][:].rearrange("p c n -> p (c n)").bitcast(E4M3X4),
                scales=w_scales[g][:].rearrange("p c n -> p (c n)"),
                in_=grouped[g][:].rearrange("p c h r u -> p (c h r u)").bitcast(BF16),
            )

        acc = {}

        def project(g, t):
            acc[g, t] = new_bank([P, HEADS, DH])
            for c in range(PASSES):
                nc.tensor.matmul_mx(
                    out=acc[g, t][:].rearrange("p h d -> p (h d)"),
                    lhsT=x_codes[:, t, c, :].bitcast(E5M2X4),
                    lhsT_scale=x_scales[:, t, c, :],
                    rhs=w_codes[g][:, c, :].bitcast(E4M3X4),
                    rhs_scale=w_scales[g][:, c, :],
                    start=(c == 0),
                    stop=(c == PASSES - 1),
                )

        spread = new_bank([P, 4, DH])

        def spread_vectors():
            nc.tensor.matmul(
                spread[:].rearrange("p a d -> p (a d)"),
                lhsT=ones[:],
                rhs=vec[:].rearrange("p a d -> p (a d)"),
                start=True,
                stop=True,
            )

        def gain_part(n, cols, scale_cols, sign):
            nc.vector.tensor_scalar(
                out=gain[n][:, cols],
                in0=spread[:, 2 * "qk".index(n), scale_cols],
                scalar1=sign,
                scalar2=sign,
                op0=ALU.mult,
                op1=ALU.add,
            )

        def gain_out1(n):
            gain_part(n, slice(0, HALF), slice(0, HALF), 1.0)
            gain_part(n, slice(HALF, DH), slice(HALF, DH), -1.0)

        def gain_out2(n):
            gain_part(n, slice(DH, 2 * DH), slice(0, DH), 1.0)

        def make_diag():
            nc.vector.tensor_tensor(
                out=diag[:],
                in0=spread[:, 1:4:2, :],
                in1=ident_bf[:].unsqueeze(1).to_broadcast([P, 2, DH]),
                op=ALU.mult,
            )

        def make_folds():
            for j, op in enumerate((ALU.subtract, ALU.add)):
                nc.vector.tensor_tensor(out=fold[:, :, j, :], in0=diag[:, :, :HALF], in1=diag[:, :, HALF:], op=op)

        def arrange_cos():
            nc.vector.tensor_copy(out=trig[:, :, 0:4:3, :], in_=cos_sb[:].rearrange("p t (j e) -> p t j e", j=2))

        def arrange_sin():
            nc.vector.tensor_copy(out=trig[:, :, 1:3, :].rearrange("p t j e -> p t (j e)"), in_=sin_sb[:])

        def make_table(engine, n, pair):
            tiles = slice(2 * pair, 2 * pair + 2)
            engine.tensor_tensor(
                out=table[n][:, tiles],
                in0=trig[:, tiles].rearrange("p t a e -> p t (a e)"),
                in1=gain[n][:].unsqueeze(1).to_broadcast([P, 2, 4 * HALF]),
                op=ALU.mult,
            )

        def turn_trig(j):
            turned["trig", j] = new_bank([P, TILES, P], BF16)
            for t in range(TILES):
                nc.tensor.transpose(
                    turned["trig", j][:, t, :],
                    trig[:, t, 2 * j : 2 * j + 2, :].rearrange("p a e -> p (a e)"),
                    ident_bf[:],
                )

        def empty_trig(j, copy):
            copy(out=trig_t[:, j], in_=turned["trig", j][:])

        def rotate_q_shifts():
            shift_ps[0] = new_bank([P, 2, 2, DH])
            for t in range(TILES):
                for j in range(2):
                    nc.tensor.matmul(
                        shift_ps[t // 2 % 2][:, t // 4, t % 2, j * HALF : (j + 1) * HALF],
                        lhsT=trig_t[:, j, t, :],
                        rhs=fold[:, 0, j, :],
                        start=True,
                        stop=True,
                    )

        def empty_even_shifts():
            nc.scalar.copy(out=shift_even_sb[:], in_=shift_ps[0][:])

        squared = {}
        sums = {}
        rstd = {}
        pair_products = {}
        tile_products = {}
        summed = {}
        stage = {}

        def squares(g, t, h0=0, h1=HEADS):
            if h0 == 0:
                squared[g, t] = work.tile([P, HEADS, DH], BF16, name="squared", tag="squared", bufs=2)
                sums[g, t] = work.tile([P, HEADS], F32, name="sums", tag="sums", bufs=4)
            for h in range(h0, h1):
                nc.scalar.activation(
                    out=squared[g, t][:, h, :],
                    in_=acc[g, t][:, h, :],
                    func=ACT.Square,
                    accum_out=sums[g, t][:, h : h + 1],
                )

        def inverse_rms(g, t):
            rstd[g, t] = work.tile([P, HEADS], F32, name="rstd", tag="rstd", bufs=4)
            nc.scalar.activation(
                out=rstd[g, t][:], in_=sums[g, t][:], func=ACT.Abs_reciprocal_sqrt, scale=1.0 / DH, bias=EPS
            )

        def multiply(g, t):
            if (g, t) in tensor_steps:
                tile_products[g, t] = work.tile(
                    [P, HEADS, 2, 2, HALF], F32, name="tile_products", tag="tile_products", bufs=3
                )
                products = tile_products[g, t][:]
            else:
                if t % 2 == 0:
                    pair_products[g, t // 2] = work.tile(
                        [P, HEADS, 2, 2, 2, HALF], F32, name="pair_products", tag="pair_products", bufs=3
                    )
                products = pair_products[g, t // 2][:, :, t % 2]
            for h in range(HEADS):
                nc.vector.scalar_tensor_tensor(
                    out=products[:, h].rearrange("p j s e -> p j (s e)"),
                    in0=acc[g, t][:, h, :].unsqueeze(1).to_broadcast([P, 2, DH]),
                    scalar=rstd[g, t][:, h : h + 1],
                    in1=table[g[0]][:, t].rearrange("p (j d) -> p j d", j=2),
                    op0=ALU.mult,
                    op1=ALU.mult,
                )

        def new_stage(g, pair):
            stage[g, pair] = work.tile([P, HEADS, 2, DH], F32, name="stage", tag="stage", bufs=5)

        def staged_tile(g, t):
            return stage[g, t // 2][:, :, t % 2, :].rearrange("p h (j e) -> p h j e", j=2)

        def store_pair(g, pair):
            nc.sync.dma_start(
                out=out_of[g][:, :, 2 * pair : 2 * pair + 2, :].rearrange("p h t d -> p h (t d)"),
                in_=stage[g, pair][:].rearrange("p h t d -> p h (t d)"),
            )

        def store_tile(g, t):
            nc.sync.dma_start(out=out_of[g][:, :, t, :], in_=stage[g, t // 2][:, :, t % 2, :])

        def add_shift(g, pair, on_gpsimd):
            engine = nc.gpsimd if on_gpsimd else nc.vector
            shift = shift_even_sb[:, pair // 2] if on_gpsimd else shift_ps[pair % 2][:, pair // 2]
            new_stage(g, pair)
            engine.tensor_tensor(
                out=stage[g, pair][:].rearrange("p h t (j e) -> p h (t j) e", j=2),
                in0=pair_products[g, pair][:, :, :, :, 0, :].rearrange("p h t j e -> p h (t j) e"),
                in1=shift.rearrange("p t (j e) -> p (t j) e", j=2).unsqueeze(1).to_broadcast([P, HEADS, 4, HALF]),
                op=ALU.add,
            )

        def add_second(g, pair):
            both = stage[g, pair][:].rearrange("p h t (j e) -> p (h t j) e", j=2)
            nc.gpsimd.tensor_tensor(
                out=both,
                in0=both,
                in1=pair_products[g, pair][:, :, :, :, 1, :].rearrange("p h t j e -> p (h t j) e"),
                op=ALU.add,
            )
            store_pair(g, pair)

        def finish_last_pair_tile(g, t):
            if t % 2 == 0:
                new_stage(g, t // 2)
            products = pair_products[g, t // 2][:, :, t % 2]
            shift = shift_ps[1][:, t // 4, t % 2, :].rearrange("p (j e) -> p j e", j=2)
            nc.vector.tensor_tensor(
                out=staged_tile(g, t),
                in0=products[:, :, :, 0, :],
                in1=shift.unsqueeze(1).to_broadcast([P, HEADS, 2, HALF]),
                op=ALU.add,
            )
            engine = nc.vector if t % 2 else nc.gpsimd
            engine.tensor_tensor(
                out=staged_tile(g, t), in0=staged_tile(g, t), in1=products[:, :, :, 1, :], op=ALU.add
            )
            store_tile(g, t)

        def tensor_add_products(g, t, s):
            nc.tensor.matmul(
                summed[g, t][:].rearrange("p h d -> p (h d)"),
                lhsT=ident_f32[:],
                rhs=tile_products[g, t][:, :, :, s, :].rearrange("p h j e -> p (h j) e"),
                start=(s == 0),
                stop=(s == 1),
            )

        def tensor_add_first(g, t):
            summed[g, t] = new_bank([P, HEADS, DH])
            tensor_add_products(g, t, 0)
            for j in range(2):
                nc.tensor.matmul(
                    summed[g, t][:, :, j * HALF : (j + 1) * HALF],
                    lhsT=trig_t[:, j, t, :],
                    rhs=fold[:, "qk".index(g[0]), j, :].unsqueeze(1).to_broadcast([P, HEADS, HALF]),
                    start=False,
                    stop=False,
                )

        def empty_result(bank, g, t):
            if t % 2 == 0:
                new_stage(g, t // 2)
            nc.scalar.copy(out=staged_tile(g, t), in_=bank[:].rearrange("p h (j e) -> p h j e", j=2))
            if g in Q_GROUPS:
                store_tile(g, t)
            elif t % 2 == 1:
                store_pair(g, t // 2)

        quant_pairs = {FIRST_LATE_PAIR + 2 * i + 1: g for i, g in enumerate(LATE_GROUPS)}
        steps = []
        pair_end = []
        k_tiles = list(range(TILES))
        for n in range(Q_PAIRS):
            g, pair = Q_GROUPS[n // (TILES // 2)], n % (TILES // 2)
            steps += [(g, 2 * pair), (g, 2 * pair + 1)]
            pair_end.append(len(steps) - 1)
            if k_tiles and n >= FIRST_LATE_PAIR and (n % 2 == 0 or n >= max(quant_pairs)):
                steps.append(("k", k_tiles.pop(0)))
        n_steps = len(steps)
        tensor_steps = {("k", t) for t in range(TILES)} | set(steps[n_steps - 4 : n_steps - 2])

        turn_x(0)
        empty_x(0)
        spread_vectors()
        make_diag()
        gain_out1("q")
        gain_out2("q")
        make_folds()
        quant_x(0)
        gain_out1("k")
        for b in range(W_BANKS):
            turn_w("q0", b)
            empty_w("q0", b)
        turn_x(1)
        empty_x(1)
        quant_w_bank("q0", 0)
        quant_w_bank("q0", 1)
        arrange_cos()
        quant_w_bank("q0", 2)
        arrange_sin()
        quant_w_bank("q0", 3)
        project("q0", 0)
        quant_x(1)
        make_table(nc.vector, "q", 0)
        turn_x(2)
        project("q0", 1)
        turn_x(3)
        make_table(nc.vector, "q", 1)
        empty_x(2, nc.vector.tensor_copy)
        quant_x(2)
        gain_out2("k")
        for n, pair in (("k", 0), ("q", 2), ("q", 3), ("k", 1), ("k", 2)):
            make_table(nc.gpsimd, n, pair)
        project("q0", 2)
        turn_x(4)
        turn_x(5)
        turn_trig(0)
        turn_trig(1)
        squares("q0", 0)
        squares("q0", 1, 0, 1)
        inverse_rms("q0", 0)
        squares("q0", 1, 1, HEADS)
        empty_x(3)
        inverse_rms("q0", 1)
        squares("q0", 2)
        empty_x(4)
        inverse_rms("q0", 2)
        empty_x(5)
        multiply("q0", 0)
        multiply("q0", 1)
        quant_x(3)
        project("q0", 3)
        turn_x(6)
        turn_x(7)
        multiply("q0", 2)
        quant_x(4, 2)
        empty_trig(0, nc.vector.tensor_copy)
        project("q0", 4)
        squares("q0", 3)
        empty_trig(1, nc.scalar.copy)
        inverse_rms("q0", 3)
        empty_x(6)
        empty_x(7)
        rotate_q_shifts()
        project("q0", 5)
        multiply("q0", 3)
        quant_x(6, 2)
        for pair in range(2):
            add_shift("q0", pair, False)
            add_second("q0", pair)
        for b in (0, 2):
            t = 4 + b // 2
            turn_w("q1", b)
            turn_w("q1", b + 1)
            project("q0", t + 2)
            squares("q0", t)
            empty_w("q1", b)
            inverse_rms("q0", t)
            empty_w("q1", b + 1)
            multiply("q0", t)
        add_shift("q0", 2, False)
        quant_w("q1")
        add_second("q0", 2)
        make_table(nc.gpsimd, "k", 3)
        for b in range(W_BANKS):
            turn_w("k", b)
        for t in (6, 7):
            b = 2 * (t - 6)
            squares("q0", t)
            empty_w("k", b)
            inverse_rms("q0", t)
            empty_w("k", b + 1)
            project(*steps[t + 2])
            multiply("q0", t)
        squares(*steps[TILES])
        empty_even_shifts()
        inverse_rms(*steps[TILES])
        squares(*steps[TILES + 1])
        quant_w("k")
        add_shift("q0", 3, False)
        add_second("q0", 3)

        late_banks = [(g, b) for g in LATE_GROUPS for b in range(W_BANKS)]
        turns = {TILES - 1 + i: late_banks[i : i + 2] for i in range(0, len(late_banks), 2)}
        quant_after = {pair_end[n]: g for n, g in quant_pairs.items()}
        v_ready = [s for s, g in quant_after.items() if g == "v"][0] + 2
        v_at = {v_ready + V_EVERY * t: t for t in range(TILES)}
        for g, b in turns.pop(TILES - 1):
            turn_w(g, b)
            empty_w(g, b)
        project(*steps[TILES + 2])

        def step_at(s):
            return steps[s] if s < n_steps else None

        for s in range(TILES, n_steps + 1):
            if step_at(s + 3):
                project(*steps[s + 3])
            if s in v_at:
                project("v", v_at[s])
            if steps[s - 2] in tensor_steps:
                tensor_add_products(*steps[s - 2], 1)
            if steps[s - 1] in tensor_steps:
                tensor_add_first(*steps[s - 1])
            for g, b in turns.get(s, []):
                turn_w(g, b)
            if step_at(s + 2):
                squares(*steps[s + 2], 0, 1)
            if step_at(s + 1):
                inverse_rms(*steps[s + 1])
            if step_at(s + 2):
                squares(*steps[s + 2], 1, HEADS)
            for g, b in turns.get(s - 1, []):
                empty_w(g, b)
            if s - 1 in v_at:
                empty_result(acc["v", v_at[s - 1]], "v", v_at[s - 1])
            if steps[s - 3] in tensor_steps:
                empty_result(summed[steps[s - 3]], *steps[s - 3])
            if step_at(s):
                multiply(*steps[s])
            if n_steps - 2 <= s < n_steps:
                finish_last_pair_tile(*steps[s])
            if s - 1 in pair_end[FIRST_LATE_PAIR : Q_PAIRS - 2]:
                g, pair = steps[s - 1][0], steps[s - 1][1] // 2
                add_shift(g, pair, pair % 2 == 0)
                if s - 1 in quant_after:
                    quant_w(quant_after[s - 1])
                add_second(g, pair)
